import numpy as np
import ml_dtypes


def mxq(x, axis, fmt="e4m3"):
    dtype, down = {"e4m3": (ml_dtypes.float8_e4m3fn, 7), "e5m2": (ml_dtypes.float8_e5m2, 14)}[fmt]
    v = np.moveaxis(np.asarray(x, np.float32).astype(ml_dtypes.bfloat16).astype(np.float64), axis, -1)
    blocks = v.reshape(v.shape[:-1] + (-1, 32))
    amax = np.abs(blocks).max(-1, keepdims=True)
    byte = np.maximum(np.where(amax > 0, np.frexp(amax)[1] - 1 + 127, 0) - down, 1)
    scale = np.exp2(byte - 127.0)
    codes = (blocks / scale).astype(np.float32).astype(dtype).astype(np.float64)
    return np.moveaxis((codes * scale).reshape(v.shape), -1, axis)


WIDE = False


def mx_kscale(k):
    if not WIDE:
        return np.ones(k)
    levels = np.array([10, -10, 5, -5, 0])
    a = np.random.permutation(np.resize(levels, k // 512 * 4)).reshape(k // 512, 4)
    idx = np.arange(k)
    return np.exp2(a[idx // 512, idx % 128 // 32])


BF16 = ml_dtypes.bfloat16


def bf(x):
    return np.asarray(x, np.float32).astype(BF16)


def f64(x):
    return np.asarray(x).astype(np.float64)


E2M1 = np.array([0.0, 0.5, 1.0, 1.5, 2.0, 3.0, 4.0, 6.0, -0.0, -0.5, -1.0, -1.5, -2.0, -3.0, -4.0, -6.0])


def pack_weight(w, fmt):
    k, n = w.shape
    w = f64(bf(w)).reshape(k // 32, 32, n)
    amax = np.abs(w).max(1)
    if fmt == "e4m3":
        byte = np.frexp(amax)[1] - 1 + 127 - 7
    else:
        mant, ex = np.frexp(amax / 6.0)
        byte = np.where(mant > 0.5, ex, ex - 1) + 127
    byte = np.clip(np.where(amax > 0, byte, 1), 1, 254)
    scaled = (w * np.exp2(127.0 - byte)[:, None, :]).reshape(k, n).astype(np.float32)
    by_word = np.ascontiguousarray(scaled.reshape(k // 512, 128, 4, n).transpose(0, 1, 3, 2))
    if fmt == "e4m3":
        words = by_word.astype(ml_dtypes.float8_e4m3fn).view(np.uint8)
    else:
        c = by_word.astype(ml_dtypes.float4_e2m1fn).view(np.uint8) & 0xF
        words = c[..., 0::2] | (c[..., 1::2] << 4)
    return np.ascontiguousarray(words), np.ascontiguousarray(byte.astype(np.uint8).reshape(k // 512, 16, n))


def unpack_weight(words, scales, fmt):
    g, p, n, _ = words.shape
    if fmt == "e4m3":
        vals = np.ascontiguousarray(words).view(ml_dtypes.float8_e4m3fn).astype(np.float64)
    else:
        nib = np.empty((g, p, n, 4), np.uint8)
        nib[..., 0::2] = words & 0xF
        nib[..., 1::2] = words >> 4
        vals = E2M1[nib]
    vals = vals * np.repeat(np.exp2(scales.astype(np.float64) - 127.0), 8, axis=1)[..., None]
    return vals.transpose(0, 1, 3, 2).reshape(g * 512, n)


NK, F, B = 3072, 512, 128
D = 2 * F
EPS = 1e-8
FMT = "e4m3"


def rotate_half(x):
    d = x.shape[-1] // 2
    return np.concatenate([-x[..., d:], x[..., :d]], axis=-1)


def setup_inputs():
    sf = mx_kscale(F)
    s = np.concatenate([sf, sf])
    c = np.exp2(np.round(0.5 * np.log2(np.mean(1.0 / s**2))))
    K = bf(np.random.standard_normal((NK, D)) * s * c)
    reference_angles = bf(np.random.random(F) * 2.0 * np.pi)
    probes = bf(np.random.standard_normal((B, D)) / s)
    u = np.random.standard_normal((B, F)) * 0.5 / np.sqrt(F) / (sf * c)
    words, scales = pack_weight(np.ascontiguousarray(u.T), FMT)
    k_bias = bf(np.random.standard_normal(B) * 0.5)
    return {"K": K,
            "reference_angles": reference_angles,
            "probes": probes,
            "u_weights_words": words,
            "u_weights_scales": scales,
            "k_bias": k_bias}


def reference(K, reference_angles, probes, u_weights_words, u_weights_scales, k_bias):
    K = f64(K)
    probes = f64(probes)
    pnorm = np.sqrt(np.sum(probes**2, axis=-1, keepdims=True))
    p = probes / (pnorm + EPS)
    theta_full = np.concatenate([f64(reference_angles), f64(reference_angles)], axis=-1)
    rotated = p * np.cos(theta_full) + rotate_half(p) * np.sin(theta_full)
    dot_term = mxq(K, 1, "e4m3") @ mxq(rotated, 1, "e4m3").T
    K_mag = np.sqrt(K[..., :F] ** 2 + K[..., F:] ** 2 + EPS)
    logits = dot_term + (mxq(K_mag, 1, "e4m3") @ unpack_weight(u_weights_words, u_weights_scales, FMT)) + f64(k_bias)
    return logits

@@ -1,0 +1,305 @@
+import math
+from contextlib import ExitStack
+
+import concourse.mybir as mybir
+from concourse.masks import make_identity
+
+F32 = mybir.dt.float32
+BF16 = mybir.dt.bfloat16
+I32 = mybir.dt.int32
+U32 = mybir.dt.uint32
+U8 = mybir.dt.uint8
+FP8X4 = mybir.dt.float8_e4m3fn_x4
+ALU = mybir.AluOpType
+ACT = mybir.ActivationFunctionType
+
+P = 128
+PACK = 4
+ROWS = 3072
+FREQS = 512
+FEATURES = 2 * FREQS
+BINS = 128
+EPS = 1e-8
+ROW_TILES = ROWS // P
+GROUP = 2
+GROUPS = ROW_TILES // GROUP
+ROUND_MAGIC = 12582912.0
+SCALAR_PLANES = 3
+ROTATE_ROUND = 1
+
+FLOPS = 2 * ROWS * BINS * (FEATURES + FREQS)
+
+
+def tile_module2network_kernel(
+    tc, K, reference_angles, probes, u_weights_words, u_weights_scales, k_bias, out
+):
+    nc = tc.nc
+    with ExitStack() as ctx:
+        const = ctx.enter_context(tc.tile_pool(name="const", bufs=1))
+        keys_pool = ctx.enter_context(tc.tile_pool(name="keys", bufs=GROUPS))
+        work = ctx.enter_context(tc.tile_pool(name="work", bufs=4))
+        codes = ctx.enter_context(tc.tile_pool(name="codes", bufs=4))
+        psum_keys = ctx.enter_context(tc.psum_pool(name="psum_keys", bufs=3))
+        psum_sums = ctx.enter_context(tc.psum_pool(name="psum_sums", bufs=3))
+        psum_out = ctx.enter_context(tc.psum_pool(name="psum_out", bufs=2))
+
+        w_scales = const.tile([P, BINS], U8, align_bytes=64)
+        nc.vector.memset(w_scales[:].bitcast(I32), 0)
+        eps_col = const.tile([P, 1], F32)
+        nc.vector.memset(eps_col[:], EPS)
+        ident = const.tile([P, P], F32)
+        make_identity(nc, ident[:])
+
+        angles = const.tile([P, 2, 2], BF16)
+        nc.scalar.dma_start(
+            out=angles[:], in_=reference_angles.rearrange("(u p e) -> p u e", u=2, e=2)
+        )
+        probes_sb = const.tile([P, FEATURES], BF16)
+        nc.sync.dma_start(out=probes_sb[:], in_=probes)
+
+        keys_dram = K.rearrange("(n r) k -> n r k", r=ROW_TILES)
+        out_dram = out.rearrange("(n r) b -> n r b", r=ROW_TILES)
+        keys = []
+
+        def load_keys(c):
+            keys_c = keys_pool.tile([P, GROUP, FEATURES], BF16)
+            nc.sync.dma_start(out=keys_c[:], in_=keys_dram[:, c * GROUP : (c + 1) * GROUP, :])
+            keys.append(keys_c)
+
+        load_keys(0)
+        load_keys(1)
+        w_codes = const.tile([P, BINS], U32, align_bytes=64)
+        nc.sync.dma_start(
+            out=w_codes[:].bitcast(I32),
+            in_=u_weights_words[0].rearrange("p n t -> p (n t)").bitcast(I32),
+        )
+        for quadrant in range(4):
+            nc.sync.dma_start(
+                out=w_scales[32 * quadrant : 32 * quadrant + 4, :].bitcast(I32),
+                in_=u_weights_scales[0, 4 * quadrant : 4 * quadrant + 4, :].bitcast(I32),
+            )
+        bias_sb = const.tile([P, BINS], BF16)
+        nc.sync.dma_start(out=bias_sb[:], in_=k_bias.partition_broadcast(P))
+        for c in range(2, GROUPS):
+            load_keys(c)
+
+        turns = const.tile([P, 2, PACK], F32)
+        angles_flat = angles[:].rearrange("p u e -> p (u e)")
+        nc.vector.tensor_scalar(
+            out=turns[:, 0, :], in0=angles_flat, scalar1=0.5 / math.pi, scalar2=None, op0=ALU.mult
+        )
+        nc.vector.tensor_scalar(
+            out=turns[:, 1, :],
+            in0=angles_flat,
+            scalar1=0.5 / math.pi,
+            scalar2=0.25,
+            op0=ALU.mult,
+            op1=ALU.add,
+        )
+        whole_turns = const.tile([P, 2, PACK], F32)
+        nc.vector.tensor_scalar(
+            out=whole_turns[:],
+            in0=turns[:],
+            scalar1=ROUND_MAGIC,
+            scalar2=ROUND_MAGIC,
+            op0=ALU.add,
+            op1=ALU.subtract,
+        )
+        part_turns = const.tile([P, 2, PACK], F32)
+        nc.vector.tensor_tensor(
+            out=part_turns[:], in0=turns[:], in1=whole_turns[:], op=ALU.subtract
+        )
+        sin_cos = const.tile([P, 2, PACK], F32)
+        nc.scalar.activation(out=sin_cos[:], in_=part_turns[:], func=ACT.Sin, scale=2.0 * math.pi)
+        sin_wide = sin_cos[:, 0, :].unsqueeze(2).to_broadcast([P, PACK, BINS])
+        cos_wide = sin_cos[:, 1, :].unsqueeze(2).to_broadcast([P, PACK, BINS])
+
+        unread = const.tile([P, FEATURES], BF16)
+        sum_squares = const.tile([P, 1], F32)
+        nc.scalar.activation(
+            out=unread[:], in_=probes_sb[:], func=ACT.Square, accum_out=sum_squares[:]
+        )
+        norm = const.tile([P, 1], F32)
+        nc.scalar.activation(out=norm[:], in_=sum_squares[:], func=ACT.Sqrt)
+        norm_eps = const.tile([P, 1], F32)
+        nc.vector.tensor_scalar_add(out=norm_eps[:], in0=norm[:], scalar1=EPS)
+        inv_norm = const.tile([P, 1], F32)
+        nc.vector.reciprocal(out=inv_norm[:], in_=norm_eps[:])
+        unit = const.tile([P, 4, 2, P], F32)
+        nc.gpsimd.tensor_scalar(
+            out=unit[:],
+            in0=probes_sb[:].rearrange("b (a p e) -> b a e p", a=4, e=2),
+            scalar1=inv_norm[:, 0:1],
+            scalar2=0.0,
+            op0=ALU.mult,
+            op1=ALU.add,
+        )
+        rotated = const.tile([P, 2, BINS, PACK], BF16, align_bytes=64)
+        rot_codes = const.tile([P, 2, BINS], U32, align_bytes=64)
+        rot_scales = const.tile([P, 2, BINS], U8, align_bytes=64)
+
+        def rotate_probes():
+            unit_planes = unit[:].rearrange("b a e p -> b (a e) p")
+            halves = []
+            for g in range(2):
+                unit_t = psum_out.tile([P, PACK, P], F32, tag="acc")
+                for t in range(PACK):
+                    nc.tensor.transpose(unit_t[:, t, :], unit_planes[:, PACK * g + t, :], ident[:])
+                halves.append(unit_t)
+            re_cos = const.tile([P, PACK, BINS], F32)
+            nc.vector.tensor_tensor(out=re_cos[:], in0=halves[0][:], in1=cos_wide, op=ALU.mult)
+            im_sin = const.tile([P, PACK, BINS], F32)
+            nc.vector.tensor_tensor(out=im_sin[:], in0=halves[1][:], in1=sin_wide, op=ALU.mult)
+            nc.gpsimd.tensor_tensor(
+                out=rotated[:, 0, :, :],
+                in0=re_cos[:].rearrange("p t b -> p b t"),
+                in1=im_sin[:].rearrange("p t b -> p b t"),
+                op=ALU.subtract,
+            )
+            im_cos = const.tile([P, PACK, BINS], F32)
+            nc.vector.tensor_tensor(out=im_cos[:], in0=halves[1][:], in1=cos_wide, op=ALU.mult)
+            re_sin = const.tile([P, PACK, BINS], F32)
+            nc.vector.tensor_tensor(out=re_sin[:], in0=halves[0][:], in1=sin_wide, op=ALU.mult)
+            nc.gpsimd.tensor_tensor(
+                out=rotated[:, 1, :, :],
+                in0=im_cos[:].rearrange("p t b -> p b t"),
+                in1=re_sin[:].rearrange("p t b -> p b t"),
+                op=ALU.add,
+            )
+
+        def quantise_probes():
+            nc.vector.quantize_mx(
+                out=rot_codes[:].rearrange("p g b -> p (g b)").bitcast(FP8X4),
+                scales=rot_scales[:].rearrange("p g b -> p (g b)"),
+                in_=rotated[:].rearrange("p g b t -> p (g b t)"),
+            )
+
+        squared = {}
+        key_words = {}
+        magnitude = {}
+        quantised = {}
+        products = {}
+
+        def square_group(c):
+            squares = work.tile([P, 2 * GROUP, PACK, P], F32)
+            by_plane = keys[c][:].rearrange("n j (h p t) -> n (j h) t p", h=2, t=PACK)
+            nc.scalar.activation(
+                out=squares[:, :, 0:SCALAR_PLANES, :],
+                in_=by_plane[:, :, 0:SCALAR_PLANES, :],
+                func=ACT.Square,
+            )
+            nc.vector.tensor_tensor(
+                out=squares[:, :, SCALAR_PLANES:PACK, :],
+                in0=by_plane[:, :, SCALAR_PLANES:PACK, :],
+                in1=by_plane[:, :, SCALAR_PLANES:PACK, :],
+                op=ALU.mult,
+            )
+            squared[c] = squares
+
+        def transpose_keys(c):
+            keys_words = work.tile([P, 2, GROUP, P, 2], F32, align_bytes=64)
+            for j in range(GROUP):
+                words = keys[c][:, j, :].bitcast(F32)
+                keys_t = psum_keys.tile([P, PACK, P], F32)
+                for a in range(PACK):
+                    nc.tensor.transpose(keys_t[:, a, :], words[:, a * P : (a + 1) * P], ident[:])
+                nc.vector.tensor_copy(
+                    out=keys_words[:, :, j, :, :],
+                    in_=keys_t[:].rearrange("p (g u) n -> p g n u", u=2),
+                )
+            key_words[c] = keys_words
+
+        def transpose_squares(c):
+            squares = squared[c]
+            magnitudes = work.tile([P, GROUP, P, PACK], BF16, align_bytes=64)
+            for j in range(GROUP):
+                sums_t = psum_sums.tile([P, PACK, P], F32)
+                for t in range(PACK):
+                    for h in range(2):
+                        nc.tensor.matmul(
+                            out=sums_t[:, t, :],
+                            lhsT=squares[:, 2 * j + h, t, :],
+                            rhs=ident[:],
+                            is_transpose=True,
+                            start=(h == 0),
+                            stop=(h == 1),
+                        )
+                nc.scalar.activation(
+                    out=magnitudes[:, j, :, :],
+                    in_=sums_t[:].rearrange("p t n -> p n t"),
+                    func=ACT.Sqrt,
+                    bias=eps_col[:, 0:1],
+                )
+            magnitude[c] = magnitudes
+
+        def quantise_group(c):
+            key_codes = codes.tile([P, 2, GROUP, P], U32, align_bytes=64)
+            key_scales = codes.tile([P, 2, GROUP, P], U8, align_bytes=64)
+            nc.vector.quantize_mx(
+                out=key_codes[:].rearrange("p g j n -> p (g j n)").bitcast(FP8X4),
+                scales=key_scales[:].rearrange("p g j n -> p (g j n)"),
+                in_=key_words[c][:].rearrange("p g j n u -> p (g j n u)").bitcast(BF16),
+            )
+            mag_codes = codes.tile([P, GROUP, P], U32, align_bytes=64)
+            mag_scales = codes.tile([P, GROUP, P], U8, align_bytes=64)
+            nc.vector.quantize_mx(
+                out=mag_codes[:].rearrange("p j n -> p (j n)").bitcast(FP8X4),
+                scales=mag_scales[:].rearrange("p j n -> p (j n)"),
+                in_=magnitude[c][:].rearrange("p j n t -> p (j n t)"),
+            )
+            quantised[c] = (key_codes, key_scales, mag_codes, mag_scales)
+
+        def multiply_group(c):
+            key_codes, key_scales, mag_codes, mag_scales = quantised[c]
+            acc = psum_out.tile([P, GROUP, BINS], F32)
+            for j in range(GROUP):
+                for g in range(2):
+                    nc.tensor.matmul_mx(
+                        out=acc[:, j, :],
+                        lhsT=key_codes[:, g, j, :].bitcast(FP8X4),
+                        lhsT_scale=key_scales[:, g, j, :],
+                        rhs=rot_codes[:, g, :].bitcast(FP8X4),
+                        rhs_scale=rot_scales[:, g, :],
+                        start=(g == 0),
+                        stop=False,
+                    )
+                nc.tensor.matmul_mx(
+                    out=acc[:, j, :],
+                    lhsT=mag_codes[:, j, :].bitcast(FP8X4),
+                    lhsT_scale=mag_scales[:, j, :],
+                    rhs=w_codes[:].bitcast(FP8X4),
+                    rhs_scale=w_scales[:],
+                    start=False,
+                    stop=True,
+                )
+            products[c] = acc
+
+        def store_group(c):
+            logits = work.tile([P, GROUP, BINS], F32)
+            nc.vector.tensor_tensor(
+                out=logits[:],
+                in0=products[c][:],
+                in1=bias_sb[:].unsqueeze(1).to_broadcast([P, GROUP, BINS]),
+                op=ALU.add,
+            )
+            nc.sync.dma_start(out=out_dram[:, c * GROUP : (c + 1) * GROUP, :], in_=logits[:])
+
+        def in_stream(c):
+            return 0 <= c < GROUPS
+
+        for i in range(GROUPS + 4):
+            if in_stream(i):
+                square_group(i)
+                transpose_keys(i)
+            if in_stream(i - 1):
+                transpose_squares(i - 1)
+            if i == ROTATE_ROUND:
+                rotate_probes()
+            if in_stream(i - 2):
+                quantise_group(i - 2)
+            if i == ROTATE_ROUND + 2:
+                quantise_probes()
+            if in_stream(i - 3):
+                multiply_group(i - 3)
+            if in_stream(i - 4):
+                store_group(i - 4)

@@ -24,7 +24,6 @@ ROW_TILES = ROWS // P
 GROUP = 2
 GROUPS = ROW_TILES // GROUP
 ROUND_MAGIC = 12582912.0
-SCALAR_PLANES = 3
 ROTATE_ROUND = 1
 
 FLOPS = 2 * ROWS * BINS * (FEATURES + FREQS)
@@ -38,9 +37,8 @@ def tile_module2network_kernel(
         const = ctx.enter_context(tc.tile_pool(name="const", bufs=1))
         keys_pool = ctx.enter_context(tc.tile_pool(name="keys", bufs=GROUPS))
         work = ctx.enter_context(tc.tile_pool(name="work", bufs=4))
-        codes = ctx.enter_context(tc.tile_pool(name="codes", bufs=4))
-        psum_keys = ctx.enter_context(tc.psum_pool(name="psum_keys", bufs=3))
-        psum_sums = ctx.enter_context(tc.psum_pool(name="psum_sums", bufs=3))
+        codes = ctx.enter_context(tc.tile_pool(name="codes", bufs=5))
+        psum_keys = ctx.enter_context(tc.psum_pool(name="psum_keys", bufs=6))
         psum_out = ctx.enter_context(tc.psum_pool(name="psum_out", bufs=2))
 
         w_scales = const.tile([P, BINS], U8, align_bytes=64)
@@ -50,10 +48,8 @@ def tile_module2network_kernel(
         ident = const.tile([P, P], F32)
         make_identity(nc, ident[:])
 
-        angles = const.tile([P, 2, 2], BF16)
-        nc.scalar.dma_start(
-            out=angles[:], in_=reference_angles.rearrange("(u p e) -> p u e", u=2, e=2)
-        )
+        angles = const.tile([P, PACK], BF16)
+        nc.scalar.dma_start(out=angles[:], in_=reference_angles.rearrange("(p t) -> p t", t=PACK))
         probes_sb = const.tile([P, FEATURES], BF16)
         nc.sync.dma_start(out=probes_sb[:], in_=probes)
 
@@ -84,7 +80,7 @@ def tile_module2network_kernel(
             load_keys(c)
 
         turns = const.tile([P, 2, PACK], F32)
-        angles_flat = angles[:].rearrange("p u e -> p (u e)")
+        angles_flat = angles[:]
         nc.vector.tensor_scalar(
             out=turns[:, 0, :], in0=angles_flat, scalar1=0.5 / math.pi, scalar2=None, op0=ALU.mult
         )
@@ -125,10 +121,10 @@ def tile_module2network_kernel(
         nc.vector.tensor_scalar_add(out=norm_eps[:], in0=norm[:], scalar1=EPS)
         inv_norm = const.tile([P, 1], F32)
         nc.vector.reciprocal(out=inv_norm[:], in_=norm_eps[:])
-        unit = const.tile([P, 4, 2, P], F32)
+        unit = const.tile([P, 2, PACK, P], F32)
         nc.gpsimd.tensor_scalar(
             out=unit[:],
-            in0=probes_sb[:].rearrange("b (a p e) -> b a e p", a=4, e=2),
+            in0=probes_sb[:].rearrange("b (g p t) -> b g t p", g=2, t=PACK),
             scalar1=inv_norm[:, 0:1],
             scalar2=0.0,
             op0=ALU.mult,
@@ -139,7 +135,7 @@ def tile_module2network_kernel(
         rot_scales = const.tile([P, 2, BINS], U8, align_bytes=64)
 
         def rotate_probes():
-            unit_planes = unit[:].rearrange("b a e p -> b (a e) p")
+            unit_planes = unit[:].rearrange("b g t p -> b (g t) p")
             halves = []
             for g in range(2):
                 unit_t = psum_out.tile([P, PACK, P], F32, tag="acc")
@@ -174,65 +170,43 @@ def tile_module2network_kernel(
                 in_=rotated[:].rearrange("p g b t -> p (g b t)"),
             )
 
-        squared = {}
         key_words = {}
+        squared = {}
+        summed = {}
         magnitude = {}
-        quantised = {}
+        key_quantised = {}
+        mag_quantised = {}
         products = {}
-
-        def square_group(c):
-            squares = work.tile([P, 2 * GROUP, PACK, P], F32)
-            by_plane = keys[c][:].rearrange("n j (h p t) -> n (j h) t p", h=2, t=PACK)
-            nc.scalar.activation(
-                out=squares[:, :, 0:SCALAR_PLANES, :],
-                in_=by_plane[:, :, 0:SCALAR_PLANES, :],
-                func=ACT.Square,
-            )
-            nc.vector.tensor_tensor(
-                out=squares[:, :, SCALAR_PLANES:PACK, :],
-                in0=by_plane[:, :, SCALAR_PLANES:PACK, :],
-                in1=by_plane[:, :, SCALAR_PLANES:PACK, :],
-                op=ALU.mult,
-            )
-            squared[c] = squares
+        GROUP_VALUES = GROUP * P * PACK
 
         def transpose_keys(c):
             keys_words = work.tile([P, 2, GROUP, P, 2], F32, align_bytes=64)
             for j in range(GROUP):
                 words = keys[c][:, j, :].bitcast(F32)
                 keys_t = psum_keys.tile([P, PACK, P], F32)
-                for a in range(PACK):
-                    nc.tensor.transpose(keys_t[:, a, :], words[:, a * P : (a + 1) * P], ident[:])
+                for g in range(2):
+                    for u in range(2):
+                        nc.tensor.transpose(
+                            keys_t[:, 2 * g + u, :],
+                            words[:, 2 * P * g + u : 2 * P * (g + 1) : 2],
+                            ident[:],
+                        )
                 nc.vector.tensor_copy(
                     out=keys_words[:, :, j, :, :],
                     in_=keys_t[:].rearrange("p (g u) n -> p g n u", u=2),
                 )
             key_words[c] = keys_words
 
-        def transpose_squares(c):
-            squares = squared[c]
-            magnitudes = work.tile([P, GROUP, P, PACK], BF16, align_bytes=64)
-            for j in range(GROUP):
-                sums_t = psum_sums.tile([P, PACK, P], F32)
-                for t in range(PACK):
-                    for h in range(2):
-                        nc.tensor.matmul(
-                            out=sums_t[:, t, :],
-                            lhsT=squares[:, 2 * j + h, t, :],
-                            rhs=ident[:],
-                            is_transpose=True,
-                            start=(h == 0),
-                            stop=(h == 1),
-                        )
-                nc.scalar.activation(
-                    out=magnitudes[:, j, :, :],
-                    in_=sums_t[:].rearrange("p t n -> p n t"),
-                    func=ACT.Sqrt,
-                    bias=eps_col[:, 0:1],
-                )
-            magnitude[c] = magnitudes
+        def square_group(c):
+            squares = work.tile([P, 2, GROUP_VALUES], F32)
+            nc.scalar.activation(
+                out=squares[:],
+                in_=key_words[c][:].rearrange("p g j n u -> p g (j n u)").bitcast(BF16),
+                func=ACT.Square,
+            )
+            squared[c] = squares
 
-        def quantise_group(c):
+        def quantise_keys(c):
             key_codes = codes.tile([P, 2, GROUP, P], U32, align_bytes=64)
             key_scales = codes.tile([P, 2, GROUP, P], U8, align_bytes=64)
             nc.vector.quantize_mx(
@@ -240,17 +214,35 @@ def tile_module2network_kernel(
                 scales=key_scales[:].rearrange("p g j n -> p (g j n)"),
                 in_=key_words[c][:].rearrange("p g j n u -> p (g j n u)").bitcast(BF16),
             )
+            key_quantised[c] = (key_codes, key_scales)
+
+        def add_group(c):
+            sums = work.tile([P, GROUP_VALUES], F32)
+            nc.vector.tensor_tensor(
+                out=sums[:], in0=squared[c][:, 0, :], in1=squared[c][:, 1, :], op=ALU.add
+            )
+            summed[c] = sums
+
+        def root_group(c):
+            magnitudes = work.tile([P, GROUP_VALUES], BF16, align_bytes=64)
+            nc.scalar.activation(
+                out=magnitudes[:], in_=summed[c][:], func=ACT.Sqrt, bias=eps_col[:, 0:1]
+            )
+            magnitude[c] = magnitudes
+
+        def quantise_magnitudes(c):
             mag_codes = codes.tile([P, GROUP, P], U32, align_bytes=64)
             mag_scales = codes.tile([P, GROUP, P], U8, align_bytes=64)
             nc.vector.quantize_mx(
                 out=mag_codes[:].rearrange("p j n -> p (j n)").bitcast(FP8X4),
                 scales=mag_scales[:].rearrange("p j n -> p (j n)"),
-                in_=magnitude[c][:].rearrange("p j n t -> p (j n t)"),
+                in_=magnitude[c][:],
             )
-            quantised[c] = (key_codes, key_scales, mag_codes, mag_scales)
+            mag_quantised[c] = (mag_codes, mag_scales)
 
         def multiply_group(c):
-            key_codes, key_scales, mag_codes, mag_scales = quantised[c]
+            key_codes, key_scales = key_quantised[c]
+            mag_codes, mag_scales = mag_quantised[c]
             acc = psum_out.tile([P, GROUP, BINS], F32)
             for j in range(GROUP):
                 for g in range(2):
@@ -287,19 +279,23 @@ def tile_module2network_kernel(
         def in_stream(c):
             return 0 <= c < GROUPS
 
-        for i in range(GROUPS + 4):
+        for i in range(GROUPS + 6):
             if in_stream(i):
-                square_group(i)
                 transpose_keys(i)
             if in_stream(i - 1):
-                transpose_squares(i - 1)
+                square_group(i - 1)
             if i == ROTATE_ROUND:
                 rotate_probes()
             if in_stream(i - 2):
-                quantise_group(i - 2)
+                quantise_keys(i - 2)
+                add_group(i - 2)
+            if in_stream(i - 3):
+                root_group(i - 3)
             if i == ROTATE_ROUND + 2:
                 quantise_probes()
-            if in_stream(i - 3):
-                multiply_group(i - 3)
             if in_stream(i - 4):
-                store_group(i - 4)
+                quantise_magnitudes(i - 4)
+            if in_stream(i - 5):
+                multiply_group(i - 5)
+            if in_stream(i - 6):
+                store_group(i - 6)

@@ -24,7 +24,9 @@ ROW_TILES = ROWS // P
 GROUP = 2
 GROUPS = ROW_TILES // GROUP
 ROUND_MAGIC = 12582912.0
-ROTATE_ROUND = 1
+SCALAR_PLANES = 3
+PSUM_ADDED_PLANES = 2
+MULTIPLY_LAG = 6
 
 FLOPS = 2 * ROWS * BINS * (FEATURES + FREQS)
 
@@ -37,9 +39,11 @@ def tile_module2network_kernel(
         const = ctx.enter_context(tc.tile_pool(name="const", bufs=1))
         keys_pool = ctx.enter_context(tc.tile_pool(name="keys", bufs=GROUPS))
         work = ctx.enter_context(tc.tile_pool(name="work", bufs=4))
-        codes = ctx.enter_context(tc.tile_pool(name="codes", bufs=5))
-        psum_keys = ctx.enter_context(tc.psum_pool(name="psum_keys", bufs=6))
+        codes = ctx.enter_context(tc.tile_pool(name="codes", bufs=MULTIPLY_LAG + 1))
+        psum_keys = ctx.enter_context(tc.psum_pool(name="psum_keys", bufs=3))
+        psum_sums = ctx.enter_context(tc.psum_pool(name="psum_sums", bufs=3))
         psum_out = ctx.enter_context(tc.psum_pool(name="psum_out", bufs=2))
+        ctx.enter_context(tc.manual_schedule())
 
         w_scales = const.tile([P, BINS], U8, align_bytes=64)
         nc.vector.memset(w_scales[:].bitcast(I32), 0)
@@ -48,10 +52,11 @@ def tile_module2network_kernel(
         ident = const.tile([P, P], F32)
         make_identity(nc, ident[:])
 
-        angles = const.tile([P, PACK], BF16)
-        nc.scalar.dma_start(out=angles[:], in_=reference_angles.rearrange("(p t) -> p t", t=PACK))
+        angles = const.tile([P, 2, 2], BF16)
+        nc.scalar.dma_start(
+            out=angles[:], in_=reference_angles.rearrange("(u p e) -> p u e", u=2, e=2)
+        )
         probes_sb = const.tile([P, FEATURES], BF16)
-        nc.sync.dma_start(out=probes_sb[:], in_=probes)
 
         keys_dram = K.rearrange("(n r) k -> n r k", r=ROW_TILES)
         out_dram = out.rearrange("(n r) b -> n r b", r=ROW_TILES)
@@ -59,11 +64,14 @@ def tile_module2network_kernel(
 
         def load_keys(c):
             keys_c = keys_pool.tile([P, GROUP, FEATURES], BF16)
-            nc.sync.dma_start(out=keys_c[:], in_=keys_dram[:, c * GROUP : (c + 1) * GROUP, :])
+            for j in range(GROUP):
+                nc.sync.dma_start(out=keys_c[:, j, :], in_=keys_dram[:, c * GROUP + j, :])
             keys.append(keys_c)
 
         load_keys(0)
-        load_keys(1)
+        nc.sync.dma_start(out=probes_sb[:], in_=probes)
+        for c in range(1, GROUPS):
+            load_keys(c)
         w_codes = const.tile([P, BINS], U32, align_bytes=64)
         nc.sync.dma_start(
             out=w_codes[:].bitcast(I32),
@@ -76,11 +84,9 @@ def tile_module2network_kernel(
             )
         bias_sb = const.tile([P, BINS], BF16)
         nc.sync.dma_start(out=bias_sb[:], in_=k_bias.partition_broadcast(P))
-        for c in range(2, GROUPS):
-            load_keys(c)
 
         turns = const.tile([P, 2, PACK], F32)
-        angles_flat = angles[:]
+        angles_flat = angles[:].rearrange("p u e -> p (u e)")
         nc.vector.tensor_scalar(
             out=turns[:, 0, :], in0=angles_flat, scalar1=0.5 / math.pi, scalar2=None, op0=ALU.mult
         )
@@ -107,60 +113,66 @@ def tile_module2network_kernel(
         )
         sin_cos = const.tile([P, 2, PACK], F32)
         nc.scalar.activation(out=sin_cos[:], in_=part_turns[:], func=ACT.Sin, scale=2.0 * math.pi)
-        sin_wide = sin_cos[:, 0, :].unsqueeze(2).to_broadcast([P, PACK, BINS])
-        cos_wide = sin_cos[:, 1, :].unsqueeze(2).to_broadcast([P, PACK, BINS])
+        sin_wide = sin_cos[:, 0, :].unsqueeze(1).to_broadcast([P, BINS, PACK])
+        cos_wide = sin_cos[:, 1, :].unsqueeze(1).to_broadcast([P, BINS, PACK])
 
-        unread = const.tile([P, FEATURES], BF16)
-        sum_squares = const.tile([P, 1], F32)
-        nc.scalar.activation(
-            out=unread[:], in_=probes_sb[:], func=ACT.Square, accum_out=sum_squares[:]
-        )
+        unit = const.tile([P, 4, 2, P], F32)
         norm = const.tile([P, 1], F32)
-        nc.scalar.activation(out=norm[:], in_=sum_squares[:], func=ACT.Sqrt)
-        norm_eps = const.tile([P, 1], F32)
-        nc.vector.tensor_scalar_add(out=norm_eps[:], in0=norm[:], scalar1=EPS)
-        inv_norm = const.tile([P, 1], F32)
-        nc.vector.reciprocal(out=inv_norm[:], in_=norm_eps[:])
-        unit = const.tile([P, 2, PACK, P], F32)
-        nc.gpsimd.tensor_scalar(
-            out=unit[:],
-            in0=probes_sb[:].rearrange("b (g p t) -> b g t p", g=2, t=PACK),
-            scalar1=inv_norm[:, 0:1],
-            scalar2=0.0,
-            op0=ALU.mult,
-            op1=ALU.add,
-        )
+        re_cos = const.tile([P, BINS, PACK], F32)
+        im_sin = const.tile([P, BINS, PACK], F32)
+        im_cos = const.tile([P, BINS, PACK], F32)
+        re_sin = const.tile([P, BINS, PACK], F32)
+
+        def normalise_probes():
+            probe_squares = const.tile([P, FEATURES], F32)
+            nc.vector.tensor_tensor(
+                out=probe_squares[:], in0=probes_sb[:], in1=probes_sb[:], op=ALU.mult
+            )
+            sum_squares = const.tile([P, 1], F32)
+            nc.vector.tensor_reduce(
+                out=sum_squares[:], in_=probe_squares[:], axis=mybir.AxisListType.X, op=ALU.add
+            )
+            nc.scalar.activation(out=norm[:], in_=sum_squares[:], func=ACT.Sqrt)
+
+        def scale_probes():
+            norm_eps = const.tile([P, 1], F32)
+            nc.vector.tensor_scalar_add(out=norm_eps[:], in0=norm[:], scalar1=EPS)
+            inv_norm = const.tile([P, 1], F32)
+            nc.vector.reciprocal(out=inv_norm[:], in_=norm_eps[:])
+            nc.gpsimd.tensor_scalar(
+                out=unit[:],
+                in0=probes_sb[:].rearrange("b (a p e) -> b a e p", a=4, e=2),
+                scalar1=inv_norm[:, 0:1],
+                scalar2=0.0,
+                op0=ALU.mult,
+                op1=ALU.add,
+            )
+
         rotated = const.tile([P, 2, BINS, PACK], BF16, align_bytes=64)
         rot_codes = const.tile([P, 2, BINS], U32, align_bytes=64)
         rot_scales = const.tile([P, 2, BINS], U8, align_bytes=64)
 
         def rotate_probes():
-            unit_planes = unit[:].rearrange("b g t p -> b (g t) p")
+            unit_planes = unit[:].rearrange("b a e p -> b (a e) p")
             halves = []
             for g in range(2):
                 unit_t = psum_out.tile([P, PACK, P], F32, tag="acc")
                 for t in range(PACK):
                     nc.tensor.transpose(unit_t[:, t, :], unit_planes[:, PACK * g + t, :], ident[:])
                 halves.append(unit_t)
-            re_cos = const.tile([P, PACK, BINS], F32)
-            nc.vector.tensor_tensor(out=re_cos[:], in0=halves[0][:], in1=cos_wide, op=ALU.mult)
-            im_sin = const.tile([P, PACK, BINS], F32)
-            nc.vector.tensor_tensor(out=im_sin[:], in0=halves[1][:], in1=sin_wide, op=ALU.mult)
+            real = halves[0][:].rearrange("p t b -> p b t")
+            imag = halves[1][:].rearrange("p t b -> p b t")
+            nc.vector.tensor_tensor(out=re_cos[:], in0=real, in1=cos_wide, op=ALU.mult)
+            nc.vector.tensor_tensor(out=re_sin[:], in0=real, in1=sin_wide, op=ALU.mult)
+            nc.vector.tensor_tensor(out=im_cos[:], in0=imag, in1=cos_wide, op=ALU.mult)
+            nc.vector.tensor_tensor(out=im_sin[:], in0=imag, in1=sin_wide, op=ALU.mult)
+
+        def combine_probes():
             nc.gpsimd.tensor_tensor(
-                out=rotated[:, 0, :, :],
-                in0=re_cos[:].rearrange("p t b -> p b t"),
-                in1=im_sin[:].rearrange("p t b -> p b t"),
-                op=ALU.subtract,
+                out=rotated[:, 0, :, :], in0=re_cos[:], in1=im_sin[:], op=ALU.subtract
             )
-            im_cos = const.tile([P, PACK, BINS], F32)
-            nc.vector.tensor_tensor(out=im_cos[:], in0=halves[1][:], in1=cos_wide, op=ALU.mult)
-            re_sin = const.tile([P, PACK, BINS], F32)
-            nc.vector.tensor_tensor(out=re_sin[:], in0=halves[0][:], in1=sin_wide, op=ALU.mult)
             nc.gpsimd.tensor_tensor(
-                out=rotated[:, 1, :, :],
-                in0=im_cos[:].rearrange("p t b -> p b t"),
-                in1=re_sin[:].rearrange("p t b -> p b t"),
-                op=ALU.add,
+                out=rotated[:, 1, :, :], in0=im_cos[:], in1=re_sin[:], op=ALU.add
             )
 
         def quantise_probes():
@@ -170,41 +182,81 @@ def tile_module2network_kernel(
                 in_=rotated[:].rearrange("p g b t -> p (g b t)"),
             )
 
-        key_words = {}
         squared = {}
-        summed = {}
+        key_words = {}
         magnitude = {}
         key_quantised = {}
         mag_quantised = {}
         products = {}
-        GROUP_VALUES = GROUP * P * PACK
+
+        def square_group(c):
+            squares = work.tile([P, 2 * GROUP, PACK, P], F32)
+            by_plane = keys[c][:].rearrange("n j (h p t) -> n (j h) t p", h=2, t=PACK)
+            nc.scalar.activation(
+                out=squares[:, :, 0:SCALAR_PLANES, :],
+                in_=by_plane[:, :, 0:SCALAR_PLANES, :],
+                func=ACT.Square,
+            )
+            nc.gpsimd.tensor_tensor(
+                out=squares[:, :, SCALAR_PLANES:PACK, :],
+                in0=by_plane[:, :, SCALAR_PLANES:PACK, :],
+                in1=by_plane[:, :, SCALAR_PLANES:PACK, :],
+                op=ALU.mult,
+            )
+            halves = squares[:].rearrange("n (j h) t p -> n j h t p", h=2)
+            nc.gpsimd.tensor_tensor(
+                out=halves[:, :, 0, SCALAR_PLANES:PACK, :],
+                in0=halves[:, :, 0, SCALAR_PLANES:PACK, :],
+                in1=halves[:, :, 1, SCALAR_PLANES:PACK, :],
+                op=ALU.add,
+            )
+            squared[c] = squares
+
+        def add_vector_plane(c):
+            halves = squared[c][:].rearrange("n (j h) t p -> n j h t p", h=2)
+            nc.vector.tensor_tensor(
+                out=halves[:, :, 0, PSUM_ADDED_PLANES:SCALAR_PLANES, :],
+                in0=halves[:, :, 0, PSUM_ADDED_PLANES:SCALAR_PLANES, :],
+                in1=halves[:, :, 1, PSUM_ADDED_PLANES:SCALAR_PLANES, :],
+                op=ALU.add,
+            )
 
         def transpose_keys(c):
             keys_words = work.tile([P, 2, GROUP, P, 2], F32, align_bytes=64)
             for j in range(GROUP):
                 words = keys[c][:, j, :].bitcast(F32)
                 keys_t = psum_keys.tile([P, PACK, P], F32)
-                for g in range(2):
-                    for u in range(2):
-                        nc.tensor.transpose(
-                            keys_t[:, 2 * g + u, :],
-                            words[:, 2 * P * g + u : 2 * P * (g + 1) : 2],
-                            ident[:],
-                        )
+                for a in range(PACK):
+                    nc.tensor.transpose(keys_t[:, a, :], words[:, a * P : (a + 1) * P], ident[:])
                 nc.vector.tensor_copy(
                     out=keys_words[:, :, j, :, :],
                     in_=keys_t[:].rearrange("p (g u) n -> p g n u", u=2),
                 )
             key_words[c] = keys_words
 
-        def square_group(c):
-            squares = work.tile([P, 2, GROUP_VALUES], F32)
-            nc.scalar.activation(
-                out=squares[:],
-                in_=key_words[c][:].rearrange("p g j n u -> p g (j n u)").bitcast(BF16),
-                func=ACT.Square,
-            )
-            squared[c] = squares
+        def transpose_squares(c):
+            squares = squared[c]
+            magnitudes = work.tile([P, GROUP, P, PACK], BF16, align_bytes=64)
+            for j in range(GROUP):
+                sums_t = psum_sums.tile([P, PACK, P], F32)
+                for t in range(PACK):
+                    parts = 2 if t < PSUM_ADDED_PLANES else 1
+                    for h in range(parts):
+                        nc.tensor.matmul(
+                            out=sums_t[:, t, :],
+                            lhsT=squares[:, 2 * j + h, t, :],
+                            rhs=ident[:],
+                            is_transpose=True,
+                            start=(h == 0),
+                            stop=(h == parts - 1),
+                        )
+                nc.scalar.activation(
+                    out=magnitudes[:, j, :, :],
+                    in_=sums_t[:].rearrange("p t n -> p n t"),
+                    func=ACT.Sqrt,
+                    bias=eps_col[:, 0:1],
+                )
+            magnitude[c] = magnitudes
 
         def quantise_keys(c):
             key_codes = codes.tile([P, 2, GROUP, P], U32, align_bytes=64)
@@ -216,27 +268,13 @@ def tile_module2network_kernel(
             )
             key_quantised[c] = (key_codes, key_scales)
 
-        def add_group(c):
-            sums = work.tile([P, GROUP_VALUES], F32)
-            nc.vector.tensor_tensor(
-                out=sums[:], in0=squared[c][:, 0, :], in1=squared[c][:, 1, :], op=ALU.add
-            )
-            summed[c] = sums
-
-        def root_group(c):
-            magnitudes = work.tile([P, GROUP_VALUES], BF16, align_bytes=64)
-            nc.scalar.activation(
-                out=magnitudes[:], in_=summed[c][:], func=ACT.Sqrt, bias=eps_col[:, 0:1]
-            )
-            magnitude[c] = magnitudes
-
         def quantise_magnitudes(c):
             mag_codes = codes.tile([P, GROUP, P], U32, align_bytes=64)
             mag_scales = codes.tile([P, GROUP, P], U8, align_bytes=64)
             nc.vector.quantize_mx(
                 out=mag_codes[:].rearrange("p j n -> p (j n)").bitcast(FP8X4),
                 scales=mag_scales[:].rearrange("p j n -> p (j n)"),
-                in_=magnitude[c][:],
+                in_=magnitude[c][:].rearrange("p j n t -> p (j n t)"),
             )
             mag_quantised[c] = (mag_codes, mag_scales)
 
@@ -279,23 +317,27 @@ def tile_module2network_kernel(
         def in_stream(c):
             return 0 <= c < GROUPS
 
-        for i in range(GROUPS + 6):
+        probe_steps = [
+            normalise_probes,
+            scale_probes,
+            rotate_probes,
+            combine_probes,
+            quantise_probes,
+        ]
+        for i in range(GROUPS + MULTIPLY_LAG + 2):
             if in_stream(i):
+                square_group(i)
                 transpose_keys(i)
             if in_stream(i - 1):
-                square_group(i - 1)
-            if i == ROTATE_ROUND:
-                rotate_probes()
+                add_vector_plane(i - 1)
+                quantise_keys(i - 1)
             if in_stream(i - 2):
-                quantise_keys(i - 2)
-                add_group(i - 2)
+                transpose_squares(i - 2)
             if in_stream(i - 3):
-                root_group(i - 3)
-            if i == ROTATE_ROUND + 2:
-                quantise_probes()
-            if in_stream(i - 4):
-                quantise_magnitudes(i - 4)
-            if in_stream(i - 5):
-                multiply_group(i - 5)
-            if in_stream(i - 6):
-                store_group(i - 6)
+                quantise_magnitudes(i - 3)
+            if 1 <= i <= len(probe_steps):
+                probe_steps[i - 1]()
+            if in_stream(i - MULTIPLY_LAG):
+                multiply_group(i - MULTIPLY_LAG)
+            if in_stream(i - MULTIPLY_LAG - 1):
+                store_group(i - MULTIPLY_LAG - 1)

@@ -25,7 +25,6 @@ GROUP = 2
 GROUPS = ROW_TILES // GROUP
 ROUND_MAGIC = 12582912.0
 SCALAR_PLANES = 3
-PSUM_ADDED_PLANES = 2
 MULTIPLY_LAG = 6
 
 FLOPS = 2 * ROWS * BINS * (FEATURES + FREQS)
@@ -203,23 +202,7 @@ def tile_module2network_kernel(
                 in1=by_plane[:, :, SCALAR_PLANES:PACK, :],
                 op=ALU.mult,
             )
-            halves = squares[:].rearrange("n (j h) t p -> n j h t p", h=2)
-            nc.gpsimd.tensor_tensor(
-                out=halves[:, :, 0, SCALAR_PLANES:PACK, :],
-                in0=halves[:, :, 0, SCALAR_PLANES:PACK, :],
-                in1=halves[:, :, 1, SCALAR_PLANES:PACK, :],
-                op=ALU.add,
-            )
             squared[c] = squares
-
-        def add_vector_plane(c):
-            halves = squared[c][:].rearrange("n (j h) t p -> n j h t p", h=2)
-            nc.vector.tensor_tensor(
-                out=halves[:, :, 0, PSUM_ADDED_PLANES:SCALAR_PLANES, :],
-                in0=halves[:, :, 0, PSUM_ADDED_PLANES:SCALAR_PLANES, :],
-                in1=halves[:, :, 1, PSUM_ADDED_PLANES:SCALAR_PLANES, :],
-                op=ALU.add,
-            )
 
         def transpose_keys(c):
             keys_words = work.tile([P, 2, GROUP, P, 2], F32, align_bytes=64)
@@ -240,15 +223,14 @@ def tile_module2network_kernel(
             for j in range(GROUP):
                 sums_t = psum_sums.tile([P, PACK, P], F32)
                 for t in range(PACK):
-                    parts = 2 if t < PSUM_ADDED_PLANES else 1
-                    for h in range(parts):
+                    for h in range(2):
                         nc.tensor.matmul(
                             out=sums_t[:, t, :],
                             lhsT=squares[:, 2 * j + h, t, :],
                             rhs=ident[:],
                             is_transpose=True,
                             start=(h == 0),
-                            stop=(h == parts - 1),
+                            stop=(h == 1),
                         )
                 nc.scalar.activation(
                     out=magnitudes[:, j, :, :],
@@ -329,7 +311,6 @@ def tile_module2network_kernel(
                 square_group(i)
                 transpose_keys(i)
             if in_stream(i - 1):
-                add_vector_plane(i - 1)
                 quantise_keys(i - 1)
             if in_stream(i - 2):
                 transpose_squares(i - 2)

@@ -25,7 +25,6 @@ GROUP = 2
 GROUPS = ROW_TILES // GROUP
 ROUND_MAGIC = 12582912.0
 SCALAR_PLANES = 3
-MULTIPLY_LAG = 6
 
 FLOPS = 2 * ROWS * BINS * (FEATURES + FREQS)
 
@@ -36,18 +35,21 @@ def tile_module2network_kernel(
     nc = tc.nc
     with ExitStack() as ctx:
         const = ctx.enter_context(tc.tile_pool(name="const", bufs=1))
-        keys_pool = ctx.enter_context(tc.tile_pool(name="keys", bufs=GROUPS))
-        work = ctx.enter_context(tc.tile_pool(name="work", bufs=4))
-        codes = ctx.enter_context(tc.tile_pool(name="codes", bufs=MULTIPLY_LAG + 1))
+        keys_pool = ctx.enter_context(tc.tile_pool(name="keys", bufs=ROW_TILES))
+        work = ctx.enter_context(tc.tile_pool(name="work", bufs=6))
+        codes = ctx.enter_context(tc.tile_pool(name="codes", bufs=6))
         psum_keys = ctx.enter_context(tc.psum_pool(name="psum_keys", bufs=3))
         psum_sums = ctx.enter_context(tc.psum_pool(name="psum_sums", bufs=3))
         psum_out = ctx.enter_context(tc.psum_pool(name="psum_out", bufs=2))
         ctx.enter_context(tc.manual_schedule())
 
-        w_scales = const.tile([P, BINS], U8, align_bytes=64)
-        nc.vector.memset(w_scales[:].bitcast(I32), 0)
         eps_col = const.tile([P, 1], F32)
         nc.vector.memset(eps_col[:], EPS)
+        quarter = const.tile([P, 2, PACK], F32)
+        nc.vector.memset(quarter[:, 0, :], 0.0)
+        nc.vector.memset(quarter[:, 1, :], 0.25)
+        w_scales = const.tile([P, BINS], U8, align_bytes=64)
+        nc.vector.memset(w_scales[:].bitcast(I32), 0)
         ident = const.tile([P, P], F32)
         make_identity(nc, ident[:])
 
@@ -55,22 +57,23 @@ def tile_module2network_kernel(
         nc.scalar.dma_start(
             out=angles[:], in_=reference_angles.rearrange("(u p e) -> p u e", u=2, e=2)
         )
+        sin_warm = const.tile([P, 1], F32)
+        nc.scalar.activation(out=sin_warm[:], in_=eps_col[:], func=ACT.Sin)
         probes_sb = const.tile([P, FEATURES], BF16)
 
         keys_dram = K.rearrange("(n r) k -> n r k", r=ROW_TILES)
         out_dram = out.rearrange("(n r) b -> n r b", r=ROW_TILES)
         keys = []
 
-        def load_keys(c):
-            keys_c = keys_pool.tile([P, GROUP, FEATURES], BF16)
-            for j in range(GROUP):
-                nc.sync.dma_start(out=keys_c[:, j, :], in_=keys_dram[:, c * GROUP + j, :])
-            keys.append(keys_c)
+        def load_keys(r):
+            keys_r = keys_pool.tile([P, FEATURES], BF16)
+            nc.sync.dma_start(out=keys_r[:], in_=keys_dram[:, r, :])
+            keys.append(keys_r)
 
         load_keys(0)
         nc.sync.dma_start(out=probes_sb[:], in_=probes)
-        for c in range(1, GROUPS):
-            load_keys(c)
+        for r in range(1, ROW_TILES):
+            load_keys(r)
         w_codes = const.tile([P, BINS], U32, align_bytes=64)
         nc.sync.dma_start(
             out=w_codes[:].bitcast(I32),
@@ -86,14 +89,11 @@ def tile_module2network_kernel(
 
         turns = const.tile([P, 2, PACK], F32)
         angles_flat = angles[:].rearrange("p u e -> p (u e)")
-        nc.vector.tensor_scalar(
-            out=turns[:, 0, :], in0=angles_flat, scalar1=0.5 / math.pi, scalar2=None, op0=ALU.mult
-        )
-        nc.vector.tensor_scalar(
-            out=turns[:, 1, :],
-            in0=angles_flat,
-            scalar1=0.5 / math.pi,
-            scalar2=0.25,
+        nc.vector.scalar_tensor_tensor(
+            out=turns[:],
+            in0=angles_flat.unsqueeze(1).to_broadcast([P, 2, PACK]),
+            scalar=0.5 / math.pi,
+            in1=quarter[:],
             op0=ALU.mult,
             op1=ALU.add,
         )
@@ -111,26 +111,39 @@ def tile_module2network_kernel(
             out=part_turns[:], in0=turns[:], in1=whole_turns[:], op=ALU.subtract
         )
         sin_cos = const.tile([P, 2, PACK], F32)
-        nc.scalar.activation(out=sin_cos[:], in_=part_turns[:], func=ACT.Sin, scale=2.0 * math.pi)
         sin_wide = sin_cos[:, 0, :].unsqueeze(1).to_broadcast([P, BINS, PACK])
         cos_wide = sin_cos[:, 1, :].unsqueeze(1).to_broadcast([P, BINS, PACK])
 
+        def take_sines():
+            nc.scalar.activation(
+                out=sin_cos[:], in_=part_turns[:], func=ACT.Sin, scale=2.0 * math.pi
+            )
+
         unit = const.tile([P, 4, 2, P], F32)
         norm = const.tile([P, 1], F32)
+        sum_squares = const.tile([P, 1], F32)
         re_cos = const.tile([P, BINS, PACK], F32)
         im_sin = const.tile([P, BINS, PACK], F32)
         im_cos = const.tile([P, BINS, PACK], F32)
         re_sin = const.tile([P, BINS, PACK], F32)
+        rotated = const.tile([P, 2, BINS, PACK], BF16, align_bytes=64)
+        rot_codes = const.tile([P, 2, BINS], U32, align_bytes=64)
+        rot_scales = const.tile([P, 2, BINS], U8, align_bytes=64)
+        transposed_probes = []
 
-        def normalise_probes():
+        def sum_probe_squares():
             probe_squares = const.tile([P, FEATURES], F32)
-            nc.vector.tensor_tensor(
-                out=probe_squares[:], in0=probes_sb[:], in1=probes_sb[:], op=ALU.mult
+            nc.vector.scalar_tensor_tensor(
+                out=probe_squares[:],
+                in0=probes_sb[:],
+                scalar=1.0,
+                in1=probes_sb[:],
+                op0=ALU.mult,
+                op1=ALU.mult,
+                accum_out=sum_squares[:],
             )
-            sum_squares = const.tile([P, 1], F32)
-            nc.vector.tensor_reduce(
-                out=sum_squares[:], in_=probe_squares[:], axis=mybir.AxisListType.X, op=ALU.add
-            )
+
+        def take_norm():
             nc.scalar.activation(out=norm[:], in_=sum_squares[:], func=ACT.Sqrt)
 
         def scale_probes():
@@ -147,24 +160,18 @@ def tile_module2network_kernel(
                 op1=ALU.add,
             )
 
-        rotated = const.tile([P, 2, BINS, PACK], BF16, align_bytes=64)
-        rot_codes = const.tile([P, 2, BINS], U32, align_bytes=64)
-        rot_scales = const.tile([P, 2, BINS], U8, align_bytes=64)
-
-        def rotate_probes():
+        def transpose_probes():
             unit_planes = unit[:].rearrange("b a e p -> b (a e) p")
-            halves = []
             for g in range(2):
                 unit_t = psum_out.tile([P, PACK, P], F32, tag="acc")
                 for t in range(PACK):
                     nc.tensor.transpose(unit_t[:, t, :], unit_planes[:, PACK * g + t, :], ident[:])
-                halves.append(unit_t)
-            real = halves[0][:].rearrange("p t b -> p b t")
-            imag = halves[1][:].rearrange("p t b -> p b t")
-            nc.vector.tensor_tensor(out=re_cos[:], in0=real, in1=cos_wide, op=ALU.mult)
-            nc.vector.tensor_tensor(out=re_sin[:], in0=real, in1=sin_wide, op=ALU.mult)
-            nc.vector.tensor_tensor(out=im_cos[:], in0=imag, in1=cos_wide, op=ALU.mult)
-            nc.vector.tensor_tensor(out=im_sin[:], in0=imag, in1=sin_wide, op=ALU.mult)
+                transposed_probes.append(unit_t[:].rearrange("p t b -> p b t"))
+
+        def rotate_half_of_probes(g, by_cos, by_sin):
+            part = transposed_probes[g]
+            nc.vector.tensor_tensor(out=by_cos[:], in0=part, in1=cos_wide, op=ALU.mult)
+            nc.vector.tensor_tensor(out=by_sin[:], in0=part, in1=sin_wide, op=ALU.mult)
 
         def combine_probes():
             nc.gpsimd.tensor_tensor(
@@ -182,63 +189,67 @@ def tile_module2network_kernel(
             )
 
         squared = {}
+        squared_by_gpsimd = {}
         key_words = {}
         magnitude = {}
         key_quantised = {}
         mag_quantised = {}
         products = {}
 
-        def square_group(c):
-            squares = work.tile([P, 2 * GROUP, PACK, P], F32)
-            by_plane = keys[c][:].rearrange("n j (h p t) -> n (j h) t p", h=2, t=PACK)
+        def planes_of(r):
+            return keys[r][:].rearrange("n (h p t) -> n h t p", h=2, t=PACK)
+
+        def square_on_scalar(r):
+            squares = work.tile([P, 2, SCALAR_PLANES, P], F32)
             nc.scalar.activation(
-                out=squares[:, :, 0:SCALAR_PLANES, :],
-                in_=by_plane[:, :, 0:SCALAR_PLANES, :],
-                func=ACT.Square,
+                out=squares[:], in_=planes_of(r)[:, :, 0:SCALAR_PLANES, :], func=ACT.Square
             )
-            nc.gpsimd.tensor_tensor(
-                out=squares[:, :, SCALAR_PLANES:PACK, :],
-                in0=by_plane[:, :, SCALAR_PLANES:PACK, :],
-                in1=by_plane[:, :, SCALAR_PLANES:PACK, :],
-                op=ALU.mult,
+            squared[r] = squares
+
+        def square_on_gpsimd(r):
+            plane = planes_of(r)[:, :, SCALAR_PLANES, :]
+            squares = work.tile([P, 2, P], F32, name="squares_gpsimd")
+            nc.gpsimd.tensor_tensor(out=squares[:], in0=plane, in1=plane, op=ALU.mult)
+            squared_by_gpsimd[r] = squares
+
+        def transpose_keys(r):
+            c, j = divmod(r, GROUP)
+            if j == 0:
+                key_words[c] = work.tile(
+                    [P, 2, GROUP, P, 2], F32, align_bytes=64, name="keys_words"
+                )
+            words = keys[r][:].bitcast(F32)
+            keys_t = psum_keys.tile([P, PACK, P], F32)
+            for a in range(PACK):
+                nc.tensor.transpose(keys_t[:, a, :], words[:, a * P : (a + 1) * P], ident[:])
+            nc.vector.tensor_copy(
+                out=key_words[c][:, :, j, :, :],
+                in_=keys_t[:].rearrange("p (g u) n -> p g n u", u=2),
             )
-            squared[c] = squares
 
-        def transpose_keys(c):
-            keys_words = work.tile([P, 2, GROUP, P, 2], F32, align_bytes=64)
-            for j in range(GROUP):
-                words = keys[c][:, j, :].bitcast(F32)
-                keys_t = psum_keys.tile([P, PACK, P], F32)
-                for a in range(PACK):
-                    nc.tensor.transpose(keys_t[:, a, :], words[:, a * P : (a + 1) * P], ident[:])
-                nc.vector.tensor_copy(
-                    out=keys_words[:, :, j, :, :],
-                    in_=keys_t[:].rearrange("p (g u) n -> p g n u", u=2),
-                )
-            key_words[c] = keys_words
-
-        def transpose_squares(c):
-            squares = squared[c]
-            magnitudes = work.tile([P, GROUP, P, PACK], BF16, align_bytes=64)
-            for j in range(GROUP):
-                sums_t = psum_sums.tile([P, PACK, P], F32)
-                for t in range(PACK):
-                    for h in range(2):
-                        nc.tensor.matmul(
-                            out=sums_t[:, t, :],
-                            lhsT=squares[:, 2 * j + h, t, :],
-                            rhs=ident[:],
-                            is_transpose=True,
-                            start=(h == 0),
-                            stop=(h == 1),
-                        )
-                nc.scalar.activation(
-                    out=magnitudes[:, j, :, :],
-                    in_=sums_t[:].rearrange("p t n -> p n t"),
-                    func=ACT.Sqrt,
-                    bias=eps_col[:, 0:1],
-                )
-            magnitude[c] = magnitudes
+        def transpose_squares(r):
+            c, j = divmod(r, GROUP)
+            if j == 0:
+                magnitude[c] = work.tile([P, GROUP, P, PACK], BF16, align_bytes=64, name="mags")
+            sums_t = psum_sums.tile([P, PACK, P], F32)
+            for t in range(PACK):
+                for h in range(2):
+                    on_scalar = t < SCALAR_PLANES
+                    square = squared[r][:, h, t, :] if on_scalar else squared_by_gpsimd[r][:, h, :]
+                    nc.tensor.matmul(
+                        out=sums_t[:, t, :],
+                        lhsT=square,
+                        rhs=ident[:],
+                        is_transpose=True,
+                        start=(h == 0),
+                        stop=(h == 1),
+                    )
+            nc.scalar.activation(
+                out=magnitude[c][:, j, :, :],
+                in_=sums_t[:].rearrange("p t n -> p n t"),
+                func=ACT.Sqrt,
+                bias=eps_col[:, 0:1],
+            )
 
         def quantise_keys(c):
             key_codes = codes.tile([P, 2, GROUP, P], U32, align_bytes=64)
@@ -296,29 +307,45 @@ def tile_module2network_kernel(
             )
             nc.sync.dma_start(out=out_dram[:, c * GROUP : (c + 1) * GROUP, :], in_=logits[:])
 
-        def in_stream(c):
-            return 0 <= c < GROUPS
-
-        probe_steps = [
-            normalise_probes,
-            scale_probes,
-            rotate_probes,
-            combine_probes,
-            quantise_probes,
-        ]
-        for i in range(GROUPS + MULTIPLY_LAG + 2):
-            if in_stream(i):
-                square_group(i)
+        AHEAD = 3
+        LAG = 3
+        FIRST_PRODUCT = 10
+        multiply_at = {}
+        for c in range(GROUPS):
+            multiply_at.setdefault(max(2 * c + LAG + 3, c + FIRST_PRODUCT), []).append(c)
+        for r in range(AHEAD):
+            square_on_gpsimd(r)
+        for i in range(ROW_TILES + LAG + 2):
+            if i < ROW_TILES:
+                square_on_scalar(i)
+            if i + AHEAD < ROW_TILES:
+                square_on_gpsimd(i + AHEAD)
+            if i == 0:
+                take_sines()
+                sum_probe_squares()
+            if i == 1:
+                take_norm()
+                scale_probes()
+            if (i - LAG) % 2 == 0 and 0 <= (i - LAG) // 2 - 1 < GROUPS:
+                quantise_magnitudes((i - LAG) // 2 - 1)
+            if 0 <= i - LAG < ROW_TILES:
+                transpose_squares(i - LAG)
+            if i < ROW_TILES:
                 transpose_keys(i)
-            if in_stream(i - 1):
-                quantise_keys(i - 1)
-            if in_stream(i - 2):
-                transpose_squares(i - 2)
-            if in_stream(i - 3):
-                quantise_magnitudes(i - 3)
-            if 1 <= i <= len(probe_steps):
-                probe_steps[i - 1]()
-            if in_stream(i - MULTIPLY_LAG):
-                multiply_group(i - MULTIPLY_LAG)
-            if in_stream(i - MULTIPLY_LAG - 1):
-                store_group(i - MULTIPLY_LAG - 1)
+            if i == 4:
+                transpose_probes()
+            if i == 5:
+                rotate_half_of_probes(0, re_cos, re_sin)
+            if i == 6:
+                rotate_half_of_probes(1, im_cos, im_sin)
+                combine_probes()
+            if i == 9:
+                quantise_probes()
+            for c in multiply_at.get(i - 1, []):
+                store_group(c)
+            if i % 2 == 0 and 0 <= i // 2 - 1 < GROUPS:
+                quantise_keys(i // 2 - 1)
+            for c in multiply_at.get(i, []):
+                multiply_group(c)
+        for c in multiply_at.get(ROW_TILES + LAG + 1, []):
+            store_group(c)

@@ -21,10 +21,20 @@ FEATURES = 2 * FREQS
 BINS = 128
 EPS = 1e-8
 ROW_TILES = ROWS // P
-GROUP = 2
-GROUPS = ROW_TILES // GROUP
+GROUP_TILES = [2, 2, 4, 4, 4, 4, 2, 1, 1]
+HALVINGS = 4
 ROUND_MAGIC = 12582912.0
 SCALAR_PLANES = 3
+
+GPSIMD_AHEAD = 3
+COPY = 1
+TRANSPOSE = 2
+ROOT = 4
+QUANTISE_KEYS = 3
+QUANTISE_MAGNITUDES = 6
+MULTIPLY = 8
+STORE = 10
+FIRST_PRODUCT = 15
 
 FLOPS = 2 * ROWS * BINS * (FEATURES + FREQS)
 
@@ -36,8 +46,9 @@ def tile_module2network_kernel(
     with ExitStack() as ctx:
         const = ctx.enter_context(tc.tile_pool(name="const", bufs=1))
         keys_pool = ctx.enter_context(tc.tile_pool(name="keys", bufs=ROW_TILES))
-        work = ctx.enter_context(tc.tile_pool(name="work", bufs=6))
-        codes = ctx.enter_context(tc.tile_pool(name="codes", bufs=6))
+        work = ctx.enter_context(tc.tile_pool(name="work", bufs=8))
+        grouped = ctx.enter_context(tc.tile_pool(name="grouped", bufs=3))
+        codes = ctx.enter_context(tc.tile_pool(name="codes", bufs=5))
         psum_keys = ctx.enter_context(tc.psum_pool(name="psum_keys", bufs=3))
         psum_sums = ctx.enter_context(tc.psum_pool(name="psum_sums", bufs=3))
         psum_out = ctx.enter_context(tc.psum_pool(name="psum_out", bufs=2))
@@ -57,8 +68,8 @@ def tile_module2network_kernel(
         nc.scalar.dma_start(
             out=angles[:], in_=reference_angles.rearrange("(u p e) -> p u e", u=2, e=2)
         )
-        sin_warm = const.tile([P, 1], F32)
-        nc.scalar.activation(out=sin_warm[:], in_=eps_col[:], func=ACT.Sin)
+        table_warm = const.tile([P, 1], F32)
+        nc.scalar.activation(out=table_warm[:], in_=eps_col[:], func=ACT.Sqrt)
         probes_sb = const.tile([P, FEATURES], BF16)
 
         keys_dram = K.rearrange("(n r) k -> n r k", r=ROW_TILES)
@@ -87,37 +98,78 @@ def tile_module2network_kernel(
         bias_sb = const.tile([P, BINS], BF16)
         nc.sync.dma_start(out=bias_sb[:], in_=k_bias.partition_broadcast(P))
 
-        turns = const.tile([P, 2, PACK], F32)
-        angles_flat = angles[:].rearrange("p u e -> p (u e)")
-        nc.vector.scalar_tensor_tensor(
-            out=turns[:],
-            in0=angles_flat.unsqueeze(1).to_broadcast([P, 2, PACK]),
-            scalar=0.5 / math.pi,
-            in1=quarter[:],
-            op0=ALU.mult,
-            op1=ALU.add,
-        )
-        whole_turns = const.tile([P, 2, PACK], F32)
-        nc.vector.tensor_scalar(
-            out=whole_turns[:],
-            in0=turns[:],
-            scalar1=ROUND_MAGIC,
-            scalar2=ROUND_MAGIC,
-            op0=ALU.add,
-            op1=ALU.subtract,
-        )
-        part_turns = const.tile([P, 2, PACK], F32)
-        nc.vector.tensor_tensor(
-            out=part_turns[:], in0=turns[:], in1=whole_turns[:], op=ALU.subtract
-        )
-        sin_cos = const.tile([P, 2, PACK], F32)
-        sin_wide = sin_cos[:, 0, :].unsqueeze(1).to_broadcast([P, BINS, PACK])
-        cos_wide = sin_cos[:, 1, :].unsqueeze(1).to_broadcast([P, BINS, PACK])
+        def small_tile(name):
+            return const.tile([P, 2, PACK], F32, name=name)
 
-        def take_sines():
-            nc.scalar.activation(
-                out=sin_cos[:], in_=part_turns[:], func=ACT.Sin, scale=2.0 * math.pi
+        turns = small_tile("turns")
+        whole_turns = small_tile("whole_turns")
+        part_turns = small_tile("part_turns")
+        z = small_tile("z")
+        cos_sin = small_tile("cos_sin")
+        cos_wide = cos_sin[:, 0, :].unsqueeze(1).to_broadcast([P, BINS, PACK])
+        sin_wide = cos_sin[:, 1, :].unsqueeze(1).to_broadcast([P, BINS, PACK])
+
+        def add_then_times(out, a, summand, b):
+            nc.vector.scalar_tensor_tensor(
+                out=out[:], in0=a[:], scalar=summand, in1=b[:], op0=ALU.add, op1=ALU.mult
             )
+
+        def take_turns():
+            nc.vector.scalar_tensor_tensor(
+                out=turns[:],
+                in0=angles[:].rearrange("p u e -> p (u e)").unsqueeze(1).to_broadcast([P, 2, PACK]),
+                scalar=0.5 / math.pi,
+                in1=quarter[:],
+                op0=ALU.mult,
+                op1=ALU.subtract,
+            )
+
+        def round_turns():
+            nc.vector.tensor_scalar(
+                out=whole_turns[:],
+                in0=turns[:],
+                scalar1=ROUND_MAGIC,
+                scalar2=ROUND_MAGIC,
+                op0=ALU.add,
+                op1=ALU.subtract,
+            )
+
+        unit_angle = 2.0 * math.pi / 2**HALVINGS
+        series = [-((-1) ** k) * unit_angle ** (2 * k) / math.factorial(2 * k) for k in range(1, 5)]
+        first_term = small_tile("first_term")
+        small_steps = [
+            take_turns,
+            round_turns,
+            lambda: nc.vector.tensor_tensor(
+                out=part_turns[:], in0=turns[:], in1=whole_turns[:], op=ALU.subtract
+            ),
+            lambda: nc.vector.tensor_tensor(
+                out=z[:], in0=part_turns[:], in1=part_turns[:], op=ALU.mult
+            ),
+            lambda: nc.vector.tensor_scalar(
+                out=first_term[:], in0=z[:], scalar1=series[3], scalar2=None, op0=ALU.mult
+            ),
+        ]
+        state = first_term
+        for k in (2, 1, 0):
+            following = small_tile("series%d" % k)
+            small_steps.append(
+                lambda out=following, a=state, k=k: add_then_times(out, a, series[k], z)
+            )
+            state = following
+        scale_of_state = 1.0
+        for k in range(HALVINGS):
+            following = small_tile("doubled%d" % k)
+            small_steps.append(
+                lambda out=following, a=state, s=-2.0 * scale_of_state: add_then_times(out, a, s, a)
+            )
+            state = following
+            scale_of_state = -0.5 * scale_of_state**2
+        small_steps.append(
+            lambda a=state, s=-1.0 / scale_of_state: nc.vector.tensor_scalar(
+                out=cos_sin[:], in0=a[:], scalar1=s, scalar2=1.0, op0=ALU.mult, op1=ALU.add
+            )
+        )
 
         unit = const.tile([P, 4, 2, P], F32)
         norm = const.tile([P, 1], F32)
@@ -146,14 +198,19 @@ def tile_module2network_kernel(
         def take_norm():
             nc.scalar.activation(out=norm[:], in_=sum_squares[:], func=ACT.Sqrt)
 
-        def scale_probes():
-            norm_eps = const.tile([P, 1], F32)
+        norm_eps = const.tile([P, 1], F32)
+        inv_norm = const.tile([P, 1], F32)
+
+        def add_eps():
             nc.vector.tensor_scalar_add(out=norm_eps[:], in0=norm[:], scalar1=EPS)
-            inv_norm = const.tile([P, 1], F32)
+
+        def invert_norm():
             nc.vector.reciprocal(out=inv_norm[:], in_=norm_eps[:])
+
+        def scale_probes(a):
             nc.gpsimd.tensor_scalar(
-                out=unit[:],
-                in0=probes_sb[:].rearrange("b (a p e) -> b a e p", a=4, e=2),
+                out=unit[:, a, :, :],
+                in0=probes_sb[:].rearrange("b (a p e) -> b a e p", a=4, e=2)[:, a, :, :],
                 scalar1=inv_norm[:, 0:1],
                 scalar2=0.0,
                 op0=ALU.mult,
@@ -173,12 +230,13 @@ def tile_module2network_kernel(
             nc.vector.tensor_tensor(out=by_cos[:], in0=part, in1=cos_wide, op=ALU.mult)
             nc.vector.tensor_tensor(out=by_sin[:], in0=part, in1=sin_wide, op=ALU.mult)
 
-        def combine_probes():
-            nc.gpsimd.tensor_tensor(
-                out=rotated[:, 0, :, :], in0=re_cos[:], in1=im_sin[:], op=ALU.subtract
+        def combine_probes(g, part):
+            half, by_cos, by_sin, op = (
+                (0, re_cos, im_sin, ALU.subtract) if g == 0 else (1, im_cos, re_sin, ALU.add)
             )
+            bins = slice(part * BINS // 2, (part + 1) * BINS // 2)
             nc.gpsimd.tensor_tensor(
-                out=rotated[:, 1, :, :], in0=im_cos[:], in1=re_sin[:], op=ALU.add
+                out=rotated[:, half, bins, :], in0=by_cos[:, bins, :], in1=by_sin[:, bins, :], op=op
             )
 
         def quantise_probes():
@@ -188,8 +246,15 @@ def tile_module2network_kernel(
                 in_=rotated[:].rearrange("p g b t -> p (g b t)"),
             )
 
+        groups = []
+        for tiles in GROUP_TILES:
+            first = sum(GROUP_TILES[: len(groups)])
+            groups.append(range(first, first + tiles))
+        place_of = {r: (c, j) for c, group in enumerate(groups) for j, r in enumerate(group)}
         squared = {}
         squared_by_gpsimd = {}
+        keys_transposed = {}
+        sums_transposed = {}
         key_words = {}
         magnitude = {}
         key_quantised = {}
@@ -213,24 +278,25 @@ def tile_module2network_kernel(
             squared_by_gpsimd[r] = squares
 
         def transpose_keys(r):
-            c, j = divmod(r, GROUP)
+            c, j = place_of[r]
             if j == 0:
-                key_words[c] = work.tile(
-                    [P, 2, GROUP, P, 2], F32, align_bytes=64, name="keys_words"
+                key_words[c] = grouped.tile(
+                    [P, 2, len(groups[c]), P, 2], F32, align_bytes=64, name="keys_words"
                 )
             words = keys[r][:].bitcast(F32)
             keys_t = psum_keys.tile([P, PACK, P], F32)
             for a in range(PACK):
                 nc.tensor.transpose(keys_t[:, a, :], words[:, a * P : (a + 1) * P], ident[:])
+            keys_transposed[r] = keys_t
+
+        def copy_keys(r):
+            c, j = place_of[r]
             nc.vector.tensor_copy(
                 out=key_words[c][:, :, j, :, :],
-                in_=keys_t[:].rearrange("p (g u) n -> p g n u", u=2),
+                in_=keys_transposed[r][:].rearrange("p (g u) n -> p g n u", u=2),
             )
 
         def transpose_squares(r):
-            c, j = divmod(r, GROUP)
-            if j == 0:
-                magnitude[c] = work.tile([P, GROUP, P, PACK], BF16, align_bytes=64, name="mags")
             sums_t = psum_sums.tile([P, PACK, P], F32)
             for t in range(PACK):
                 for h in range(2):
@@ -244,16 +310,25 @@ def tile_module2network_kernel(
                         start=(h == 0),
                         stop=(h == 1),
                     )
+            sums_transposed[r] = sums_t
+
+        def take_roots(r):
+            c, j = place_of[r]
+            if j == 0:
+                magnitude[c] = grouped.tile(
+                    [P, len(groups[c]), P, PACK], BF16, align_bytes=64, name="mags"
+                )
             nc.scalar.activation(
                 out=magnitude[c][:, j, :, :],
-                in_=sums_t[:].rearrange("p t n -> p n t"),
+                in_=sums_transposed[r][:].rearrange("p t n -> p n t"),
                 func=ACT.Sqrt,
                 bias=eps_col[:, 0:1],
             )
 
         def quantise_keys(c):
-            key_codes = codes.tile([P, 2, GROUP, P], U32, align_bytes=64)
-            key_scales = codes.tile([P, 2, GROUP, P], U8, align_bytes=64)
+            tiles = len(groups[c])
+            key_codes = codes.tile([P, 2, tiles, P], U32, align_bytes=64)
+            key_scales = codes.tile([P, 2, tiles, P], U8, align_bytes=64)
             nc.vector.quantize_mx(
                 out=key_codes[:].rearrange("p g j n -> p (g j n)").bitcast(FP8X4),
                 scales=key_scales[:].rearrange("p g j n -> p (g j n)"),
@@ -262,8 +337,9 @@ def tile_module2network_kernel(
             key_quantised[c] = (key_codes, key_scales)
 
         def quantise_magnitudes(c):
-            mag_codes = codes.tile([P, GROUP, P], U32, align_bytes=64)
-            mag_scales = codes.tile([P, GROUP, P], U8, align_bytes=64)
+            tiles = len(groups[c])
+            mag_codes = codes.tile([P, tiles, P], U32, align_bytes=64)
+            mag_scales = codes.tile([P, tiles, P], U8, align_bytes=64)
             nc.vector.quantize_mx(
                 out=mag_codes[:].rearrange("p j n -> p (j n)").bitcast(FP8X4),
                 scales=mag_scales[:].rearrange("p j n -> p (j n)"),
@@ -274,8 +350,9 @@ def tile_module2network_kernel(
         def multiply_group(c):
             key_codes, key_scales = key_quantised[c]
             mag_codes, mag_scales = mag_quantised[c]
-            acc = psum_out.tile([P, GROUP, BINS], F32)
-            for j in range(GROUP):
+            tiles = len(groups[c])
+            acc = psum_out.tile([P, tiles, BINS], F32)
+            for j in range(tiles):
                 for g in range(2):
                     nc.tensor.matmul_mx(
                         out=acc[:, j, :],
@@ -298,54 +375,81 @@ def tile_module2network_kernel(
             products[c] = acc
 
         def store_group(c):
-            logits = work.tile([P, GROUP, BINS], F32)
+            first, tiles = groups[c][0], len(groups[c])
+            logits = work.tile([P, tiles, BINS], F32)
             nc.vector.tensor_tensor(
                 out=logits[:],
                 in0=products[c][:],
-                in1=bias_sb[:].unsqueeze(1).to_broadcast([P, GROUP, BINS]),
+                in1=bias_sb[:].unsqueeze(1).to_broadcast([P, tiles, BINS]),
                 op=ALU.add,
             )
-            nc.sync.dma_start(out=out_dram[:, c * GROUP : (c + 1) * GROUP, :], in_=logits[:])
+            nc.sync.dma_start(out=out_dram[:, first : first + tiles, :], in_=logits[:])
 
-        AHEAD = 3
-        LAG = 3
-        FIRST_PRODUCT = 10
-        multiply_at = {}
-        for c in range(GROUPS):
-            multiply_at.setdefault(max(2 * c + LAG + 3, c + FIRST_PRODUCT), []).append(c)
-        for r in range(AHEAD):
+        def tile_at(i, lag):
+            return i - lag if 0 <= i - lag < ROW_TILES else None
+
+        groups_at = {}
+        previous = FIRST_PRODUCT - 1
+        for c, group in enumerate(groups):
+            last = group[-1]
+            groups_at.setdefault((quantise_keys, last + QUANTISE_KEYS), []).append(c)
+            groups_at.setdefault((quantise_magnitudes, last + QUANTISE_MAGNITUDES), []).append(c)
+            previous = max(last + MULTIPLY, previous + 1)
+            groups_at.setdefault((multiply_group, previous), []).append(c)
+            groups_at.setdefault((store_group, previous + STORE - MULTIPLY), []).append(c)
+
+        def groups_do(stage, i):
+            for c in groups_at.get((stage, i), []):
+                stage(c)
+
+        def next_small_step():
+            if small_steps:
+                small_steps.pop(0)()
+
+        for r in range(GPSIMD_AHEAD):
             square_on_gpsimd(r)
-        for i in range(ROW_TILES + LAG + 2):
-            if i < ROW_TILES:
+        for i in range(ROW_TILES + STORE + 8):
+            if tile_at(i, 0) is not None:
                 square_on_scalar(i)
-            if i + AHEAD < ROW_TILES:
-                square_on_gpsimd(i + AHEAD)
+            if tile_at(i, -GPSIMD_AHEAD) is not None:
+                square_on_gpsimd(i + GPSIMD_AHEAD)
             if i == 0:
-                take_sines()
+                for k in range(4):
+                    next_small_step()
                 sum_probe_squares()
-            if i == 1:
+            if i == 3:
                 take_norm()
-                scale_probes()
-            if (i - LAG) % 2 == 0 and 0 <= (i - LAG) // 2 - 1 < GROUPS:
-                quantise_magnitudes((i - LAG) // 2 - 1)
-            if 0 <= i - LAG < ROW_TILES:
-                transpose_squares(i - LAG)
-            if i < ROW_TILES:
+            if tile_at(i, 0) is not None:
                 transpose_keys(i)
+            groups_do(quantise_magnitudes, i)
+            if i == 3:
+                add_eps()
+            if tile_at(i, COPY) is not None:
+                copy_keys(i - COPY)
+            if i == 3:
+                invert_norm()
+            else:
+                next_small_step()
+            groups_do(store_group, i)
             if i == 4:
+                for a in range(4):
+                    scale_probes(a)
+            groups_do(quantise_keys, i)
+            if (quantise_keys, i) in groups_at:
+                next_small_step()
+            if tile_at(i, ROOT) is not None:
+                take_roots(i - ROOT)
+            if tile_at(i, TRANSPOSE) is not None:
+                transpose_squares(i - TRANSPOSE)
+            if i == 7:
                 transpose_probes()
-            if i == 5:
-                rotate_half_of_probes(0, re_cos, re_sin)
-            if i == 6:
-                rotate_half_of_probes(1, im_cos, im_sin)
-                combine_probes()
             if i == 9:
+                rotate_half_of_probes(0, re_cos, re_sin)
+            if i == 9:
+                rotate_half_of_probes(1, im_cos, im_sin)
+            if 10 <= i < 12:
+                for part in range(2):
+                    combine_probes(i - 10, part)
+            if i == 14:
                 quantise_probes()
-            for c in multiply_at.get(i - 1, []):
-                store_group(c)
-            if i % 2 == 0 and 0 <= i // 2 - 1 < GROUPS:
-                quantise_keys(i // 2 - 1)
-            for c in multiply_at.get(i, []):
-                multiply_group(c)
-        for c in multiply_at.get(ROW_TILES + LAG + 1, []):
-            store_group(c)
+            groups_do(multiply_group, i)

@@ -24,7 +24,7 @@ ROW_TILES = ROWS // P
 GROUP_TILES = [2, 2, 4, 4, 4, 4, 2, 1, 1]
 HALVINGS = 4
 ROUND_MAGIC = 12582912.0
-SCALAR_PLANES = 3
+SCALAR_ALONE_EVERY = 3
 
 GPSIMD_AHEAD = 3
 COPY = 1
@@ -264,15 +264,21 @@ def tile_module2network_kernel(
         def planes_of(r):
             return keys[r][:].rearrange("n (h p t) -> n h t p", h=2, t=PACK)
 
+        def scalar_planes(r):
+            return PACK - 1 if r % SCALAR_ALONE_EVERY else PACK
+
         def square_on_scalar(r):
-            squares = work.tile([P, 2, SCALAR_PLANES, P], F32)
+            planes = scalar_planes(r)
+            squares = work.tile([P, 2, planes, P], F32, name="squares")
             nc.scalar.activation(
-                out=squares[:], in_=planes_of(r)[:, :, 0:SCALAR_PLANES, :], func=ACT.Square
+                out=squares[:], in_=planes_of(r)[:, :, 0:planes, :], func=ACT.Square
             )
             squared[r] = squares
 
         def square_on_gpsimd(r):
-            plane = planes_of(r)[:, :, SCALAR_PLANES, :]
+            if scalar_planes(r) == PACK:
+                return
+            plane = planes_of(r)[:, :, PACK - 1, :]
             squares = work.tile([P, 2, P], F32, name="squares_gpsimd")
             nc.gpsimd.tensor_tensor(out=squares[:], in0=plane, in1=plane, op=ALU.mult)
             squared_by_gpsimd[r] = squares
@@ -300,7 +306,7 @@ def tile_module2network_kernel(
             sums_t = psum_sums.tile([P, PACK, P], F32)
             for t in range(PACK):
                 for h in range(2):
-                    on_scalar = t < SCALAR_PLANES
+                    on_scalar = t < scalar_planes(r)
                     square = squared[r][:, h, t, :] if on_scalar else squared_by_gpsimd[r][:, h, :]
                     nc.tensor.matmul(
                         out=sums_t[:, t, :],

@@ -22,6 +22,8 @@ BINS = 128
 EPS = 1e-8
 ROW_TILES = ROWS // P
 GROUP_TILES = [2, 2, 4, 4, 4, 4, 2, 1, 1]
+CLOCK_AT_START = 4
+CLOCK_TWICE = 8
 HALVINGS = 4
 ROUND_MAGIC = 12582912.0
 SCALAR_ALONE_EVERY = 3
@@ -283,6 +285,12 @@ def tile_module2network_kernel(
             nc.gpsimd.tensor_tensor(out=squares[:], in0=plane, in1=plane, op=ALU.mult)
             squared_by_gpsimd[r] = squares
 
+        def keep_clock(out):
+            nc.tensor.matmul(out=out, lhsT=ident[:], rhs=ident[:], start=True, stop=True)
+
+        def clock_products(r):
+            return (r < CLOCK_TWICE) + (r < FIRST_PRODUCT)
+
         def transpose_keys(r):
             c, j = place_of[r]
             if j == 0:
@@ -291,6 +299,9 @@ def tile_module2network_kernel(
                 )
             words = keys[r][:].bitcast(F32)
             keys_t = psum_keys.tile([P, PACK, P], F32)
+            if r == 0:
+                for a in range(CLOCK_AT_START):
+                    keep_clock(keys_t[:, a, :])
             for a in range(PACK):
                 nc.tensor.transpose(keys_t[:, a, :], words[:, a * P : (a + 1) * P], ident[:])
             keys_transposed[r] = keys_t
@@ -304,6 +315,8 @@ def tile_module2network_kernel(
 
         def transpose_squares(r):
             sums_t = psum_sums.tile([P, PACK, P], F32)
+            for t in range(clock_products(r)):
+                keep_clock(sums_t[:, t, :])
             for t in range(PACK):
                 for h in range(2):
                     on_scalar = t < scalar_planes(r)

@@ -23,7 +23,7 @@ EPS = 1e-8
 ROW_TILES = ROWS // P
 GROUP_TILES = [2, 2, 4, 4, 4, 4, 2, 1, 1]
 CLOCK_AT_START = 4
-CLOCK_TWICE = 8
+CLOCK_TWICE = 4
 HALVINGS = 4
 ROUND_MAGIC = 12582912.0
 SCALAR_ALONE_EVERY = 3
@@ -36,7 +36,7 @@ QUANTISE_KEYS = 3
 QUANTISE_MAGNITUDES = 6
 MULTIPLY = 8
 STORE = 10
-FIRST_PRODUCT = 15
+FIRST_PRODUCT = 14
 
 FLOPS = 2 * ROWS * BINS * (FEATURES + FREQS)
 
@@ -436,21 +436,21 @@ def tile_module2network_kernel(
                 for k in range(4):
                     next_small_step()
                 sum_probe_squares()
-            if i == 3:
+            if i == 2:
                 take_norm()
             if tile_at(i, 0) is not None:
                 transpose_keys(i)
             groups_do(quantise_magnitudes, i)
-            if i == 3:
+            if i == 2:
                 add_eps()
             if tile_at(i, COPY) is not None:
                 copy_keys(i - COPY)
-            if i == 3:
+            if i == 2:
                 invert_norm()
             else:
                 next_small_step()
             groups_do(store_group, i)
-            if i == 4:
+            if i == 3:
                 for a in range(4):
                     scale_probes(a)
             groups_do(quantise_keys, i)
@@ -460,15 +460,15 @@ def tile_module2network_kernel(
                 take_roots(i - ROOT)
             if tile_at(i, TRANSPOSE) is not None:
                 transpose_squares(i - TRANSPOSE)
-            if i == 7:
+            if i == 6:
                 transpose_probes()
-            if i == 9:
+            if i == 8:
                 rotate_half_of_probes(0, re_cos, re_sin)
-            if i == 9:
+            if i == 8:
                 rotate_half_of_probes(1, im_cos, im_sin)
-            if 10 <= i < 12:
+            if 9 <= i < 11:
                 for part in range(2):
-                    combine_probes(i - 10, part)
-            if i == 14:
+                    combine_probes(i - 9, part)
+            if i == 13:
                 quantise_probes()
             groups_do(multiply_group, i)

import math
from contextlib import ExitStack

import concourse.mybir as mybir
from concourse.masks import make_identity

F32 = mybir.dt.float32
BF16 = mybir.dt.bfloat16
I32 = mybir.dt.int32
U32 = mybir.dt.uint32
U8 = mybir.dt.uint8
FP8X4 = mybir.dt.float8_e4m3fn_x4
ALU = mybir.AluOpType
ACT = mybir.ActivationFunctionType

P = 128
PACK = 4
ROWS = 3072
FREQS = 512
FEATURES = 2 * FREQS
BINS = 128
EPS = 1e-8
ROW_TILES = ROWS // P
GROUP_TILES = [2, 2, 4, 4, 4, 4, 2, 1, 1]
CLOCK_AT_START = 4
CLOCK_TWICE = 4
HALVINGS = 4
ROUND_MAGIC = 12582912.0
SCALAR_ALONE_EVERY = 3

GPSIMD_AHEAD = 3
COPY = 1
TRANSPOSE = 2
ROOT = 4
QUANTISE_KEYS = 3
QUANTISE_MAGNITUDES = 6
MULTIPLY = 8
STORE = 10
FIRST_PRODUCT = 14

FLOPS = 2 * ROWS * BINS * (FEATURES + FREQS)


def tile_module2network_kernel(
    tc, K, reference_angles, probes, u_weights_words, u_weights_scales, k_bias, out
):
    nc = tc.nc
    with ExitStack() as ctx:
        const = ctx.enter_context(tc.tile_pool(name="const", bufs=1))
        keys_pool = ctx.enter_context(tc.tile_pool(name="keys", bufs=ROW_TILES))
        work = ctx.enter_context(tc.tile_pool(name="work", bufs=8))
        grouped = ctx.enter_context(tc.tile_pool(name="grouped", bufs=3))
        codes = ctx.enter_context(tc.tile_pool(name="codes", bufs=5))
        psum_keys = ctx.enter_context(tc.psum_pool(name="psum_keys", bufs=3))
        psum_sums = ctx.enter_context(tc.psum_pool(name="psum_sums", bufs=3))
        psum_out = ctx.enter_context(tc.psum_pool(name="psum_out", bufs=2))
        ctx.enter_context(tc.manual_schedule())

        eps_col = const.tile([P, 1], F32)
        nc.vector.memset(eps_col[:], EPS)
        quarter = const.tile([P, 2, PACK], F32)
        nc.vector.memset(quarter[:, 0, :], 0.0)
        nc.vector.memset(quarter[:, 1, :], 0.25)
        w_scales = const.tile([P, BINS], U8, align_bytes=64)
        nc.vector.memset(w_scales[:].bitcast(I32), 0)
        ident = const.tile([P, P], F32)
        make_identity(nc, ident[:])

        angles = const.tile([P, 2, 2], BF16)
        nc.scalar.dma_start(
            out=angles[:], in_=reference_angles.rearrange("(u p e) -> p u e", u=2, e=2)
        )
        table_warm = const.tile([P, 1], F32)
        nc.scalar.activation(out=table_warm[:], in_=eps_col[:], func=ACT.Sqrt)
        probes_sb = const.tile([P, FEATURES], BF16)

        keys_dram = K.rearrange("(n r) k -> n r k", r=ROW_TILES)
        out_dram = out.rearrange("(n r) b -> n r b", r=ROW_TILES)
        keys = []

        def load_keys(r):
            keys_r = keys_pool.tile([P, FEATURES], BF16)
            nc.sync.dma_start(out=keys_r[:], in_=keys_dram[:, r, :])
            keys.append(keys_r)

        load_keys(0)
        nc.sync.dma_start(out=probes_sb[:], in_=probes)
        for r in range(1, ROW_TILES):
            load_keys(r)
        w_codes = const.tile([P, BINS], U32, align_bytes=64)
        nc.sync.dma_start(
            out=w_codes[:].bitcast(I32),
            in_=u_weights_words[0].rearrange("p n t -> p (n t)").bitcast(I32),
        )
        for quadrant in range(4):
            nc.sync.dma_start(
                out=w_scales[32 * quadrant : 32 * quadrant + 4, :].bitcast(I32),
                in_=u_weights_scales[0, 4 * quadrant : 4 * quadrant + 4, :].bitcast(I32),
            )
        bias_sb = const.tile([P, BINS], BF16)
        nc.sync.dma_start(out=bias_sb[:], in_=k_bias.partition_broadcast(P))

        def small_tile(name):
            return const.tile([P, 2, PACK], F32, name=name)

        turns = small_tile("turns")
        whole_turns = small_tile("whole_turns")
        part_turns = small_tile("part_turns")
        z = small_tile("z")
        cos_sin = small_tile("cos_sin")
        cos_wide = cos_sin[:, 0, :].unsqueeze(1).to_broadcast([P, BINS, PACK])
        sin_wide = cos_sin[:, 1, :].unsqueeze(1).to_broadcast([P, BINS, PACK])

        def add_then_times(out, a, summand, b):
            nc.vector.scalar_tensor_tensor(
                out=out[:], in0=a[:], scalar=summand, in1=b[:], op0=ALU.add, op1=ALU.mult
            )

        def take_turns():
            nc.vector.scalar_tensor_tensor(
                out=turns[:],
                in0=angles[:].rearrange("p u e -> p (u e)").unsqueeze(1).to_broadcast([P, 2, PACK]),
                scalar=0.5 / math.pi,
                in1=quarter[:],
                op0=ALU.mult,
                op1=ALU.subtract,
            )

        def round_turns():
            nc.vector.tensor_scalar(
                out=whole_turns[:],
                in0=turns[:],
                scalar1=ROUND_MAGIC,
                scalar2=ROUND_MAGIC,
                op0=ALU.add,
                op1=ALU.subtract,
            )

        unit_angle = 2.0 * math.pi / 2**HALVINGS
        series = [-((-1) ** k) * unit_angle ** (2 * k) / math.factorial(2 * k) for k in range(1, 5)]
        first_term = small_tile("first_term")
        small_steps = [
            take_turns,
            round_turns,
            lambda: nc.vector.tensor_tensor(
                out=part_turns[:], in0=turns[:], in1=whole_turns[:], op=ALU.subtract
            ),
            lambda: nc.vector.tensor_tensor(
                out=z[:], in0=part_turns[:], in1=part_turns[:], op=ALU.mult
            ),
            lambda: nc.vector.tensor_scalar(
                out=first_term[:], in0=z[:], scalar1=series[3], scalar2=None, op0=ALU.mult
            ),
        ]
        state = first_term
        for k in (2, 1, 0):
            following = small_tile("series%d" % k)
            small_steps.append(
                lambda out=following, a=state, k=k: add_then_times(out, a, series[k], z)
            )
            state = following
        scale_of_state = 1.0
        for k in range(HALVINGS):
            following = small_tile("doubled%d" % k)
            small_steps.append(
                lambda out=following, a=state, s=-2.0 * scale_of_state: add_then_times(out, a, s, a)
            )
            state = following
            scale_of_state = -0.5 * scale_of_state**2
        small_steps.append(
            lambda a=state, s=-1.0 / scale_of_state: nc.vector.tensor_scalar(
                out=cos_sin[:], in0=a[:], scalar1=s, scalar2=1.0, op0=ALU.mult, op1=ALU.add
            )
        )

        unit = const.tile([P, 4, 2, P], F32)
        norm = const.tile([P, 1], F32)
        sum_squares = const.tile([P, 1], F32)
        re_cos = const.tile([P, BINS, PACK], F32)
        im_sin = const.tile([P, BINS, PACK], F32)
        im_cos = const.tile([P, BINS, PACK], F32)
        re_sin = const.tile([P, BINS, PACK], F32)
        rotated = const.tile([P, 2, BINS, PACK], BF16, align_bytes=64)
        rot_codes = const.tile([P, 2, BINS], U32, align_bytes=64)
        rot_scales = const.tile([P, 2, BINS], U8, align_bytes=64)
        transposed_probes = []

        def sum_probe_squares():
            probe_squares = const.tile([P, FEATURES], F32)
            nc.vector.scalar_tensor_tensor(
                out=probe_squares[:],
                in0=probes_sb[:],
                scalar=1.0,
                in1=probes_sb[:],
                op0=ALU.mult,
                op1=ALU.mult,
                accum_out=sum_squares[:],
            )

        def take_norm():
            nc.scalar.activation(out=norm[:], in_=sum_squares[:], func=ACT.Sqrt)

        norm_eps = const.tile([P, 1], F32)
        inv_norm = const.tile([P, 1], F32)

        def add_eps():
            nc.vector.tensor_scalar_add(out=norm_eps[:], in0=norm[:], scalar1=EPS)

        def invert_norm():
            nc.vector.reciprocal(out=inv_norm[:], in_=norm_eps[:])

        def scale_probes(a):
            nc.gpsimd.tensor_scalar(
                out=unit[:, a, :, :],
                in0=probes_sb[:].rearrange("b (a p e) -> b a e p", a=4, e=2)[:, a, :, :],
                scalar1=inv_norm[:, 0:1],
                scalar2=0.0,
                op0=ALU.mult,
                op1=ALU.add,
            )

        def transpose_probes():
            unit_planes = unit[:].rearrange("b a e p -> b (a e) p")
            for g in range(2):
                unit_t = psum_out.tile([P, PACK, P], F32, tag="acc")
                for t in range(PACK):
                    nc.tensor.transpose(unit_t[:, t, :], unit_planes[:, PACK * g + t, :], ident[:])
                transposed_probes.append(unit_t[:].rearrange("p t b -> p b t"))

        def rotate_half_of_probes(g, by_cos, by_sin):
            part = transposed_probes[g]
            nc.vector.tensor_tensor(out=by_cos[:], in0=part, in1=cos_wide, op=ALU.mult)
            nc.vector.tensor_tensor(out=by_sin[:], in0=part, in1=sin_wide, op=ALU.mult)

        def combine_probes(g, part):
            half, by_cos, by_sin, op = (
                (0, re_cos, im_sin, ALU.subtract) if g == 0 else (1, im_cos, re_sin, ALU.add)
            )
            bins = slice(part * BINS // 2, (part + 1) * BINS // 2)
            nc.gpsimd.tensor_tensor(
                out=rotated[:, half, bins, :], in0=by_cos[:, bins, :], in1=by_sin[:, bins, :], op=op
            )

        def quantise_probes():
            nc.vector.quantize_mx(
                out=rot_codes[:].rearrange("p g b -> p (g b)").bitcast(FP8X4),
                scales=rot_scales[:].rearrange("p g b -> p (g b)"),
                in_=rotated[:].rearrange("p g b t -> p (g b t)"),
            )

        groups = []
        for tiles in GROUP_TILES:
            first = sum(GROUP_TILES[: len(groups)])
            groups.append(range(first, first + tiles))
        place_of = {r: (c, j) for c, group in enumerate(groups) for j, r in enumerate(group)}
        squared = {}
        squared_by_gpsimd = {}
        keys_transposed = {}
        sums_transposed = {}
        key_words = {}
        magnitude = {}
        key_quantised = {}
        mag_quantised = {}
        products = {}

        def planes_of(r):
            return keys[r][:].rearrange("n (h p t) -> n h t p", h=2, t=PACK)

        def scalar_planes(r):
            return PACK - 1 if r % SCALAR_ALONE_EVERY else PACK

        def square_on_scalar(r):
            planes = scalar_planes(r)
            squares = work.tile([P, 2, planes, P], F32, name="squares")
            nc.scalar.activation(
                out=squares[:], in_=planes_of(r)[:, :, 0:planes, :], func=ACT.Square
            )
            squared[r] = squares

        def square_on_gpsimd(r):
            if scalar_planes(r) == PACK:
                return
            plane = planes_of(r)[:, :, PACK - 1, :]
            squares = work.tile([P, 2, P], F32, name="squares_gpsimd")
            nc.gpsimd.tensor_tensor(out=squares[:], in0=plane, in1=plane, op=ALU.mult)
            squared_by_gpsimd[r] = squares

        def keep_clock(out):
            nc.tensor.matmul(out=out, lhsT=ident[:], rhs=ident[:], start=True, stop=True)

        def clock_products(r):
            return (r < CLOCK_TWICE) + (r < FIRST_PRODUCT)

        def transpose_keys(r):
            c, j = place_of[r]
            if j == 0:
                key_words[c] = grouped.tile(
                    [P, 2, len(groups[c]), P, 2], F32, align_bytes=64, name="keys_words"
                )
            words = keys[r][:].bitcast(F32)
            keys_t = psum_keys.tile([P, PACK, P], F32)
            if r == 0:
                for a in range(CLOCK_AT_START):
                    keep_clock(keys_t[:, a, :])
            for a in range(PACK):
                nc.tensor.transpose(keys_t[:, a, :], words[:, a * P : (a + 1) * P], ident[:])
            keys_transposed[r] = keys_t

        def copy_keys(r):
            c, j = place_of[r]
            nc.vector.tensor_copy(
                out=key_words[c][:, :, j, :, :],
                in_=keys_transposed[r][:].rearrange("p (g u) n -> p g n u", u=2),
            )

        def transpose_squares(r):
            sums_t = psum_sums.tile([P, PACK, P], F32)
            for t in range(clock_products(r)):
                keep_clock(sums_t[:, t, :])
            for t in range(PACK):
                for h in range(2):
                    on_scalar = t < scalar_planes(r)
                    square = squared[r][:, h, t, :] if on_scalar else squared_by_gpsimd[r][:, h, :]
                    nc.tensor.matmul(
                        out=sums_t[:, t, :],
                        lhsT=square,
                        rhs=ident[:],
                        is_transpose=True,
                        start=(h == 0),
                        stop=(h == 1),
                    )
            sums_transposed[r] = sums_t

        def take_roots(r):
            c, j = place_of[r]
            if j == 0:
                magnitude[c] = grouped.tile(
                    [P, len(groups[c]), P, PACK], BF16, align_bytes=64, name="mags"
                )
            nc.scalar.activation(
                out=magnitude[c][:, j, :, :],
                in_=sums_transposed[r][:].rearrange("p t n -> p n t"),
                func=ACT.Sqrt,
                bias=eps_col[:, 0:1],
            )

        def quantise_keys(c):
            tiles = len(groups[c])
            key_codes = codes.tile([P, 2, tiles, P], U32, align_bytes=64)
            key_scales = codes.tile([P, 2, tiles, P], U8, align_bytes=64)
            nc.vector.quantize_mx(
                out=key_codes[:].rearrange("p g j n -> p (g j n)").bitcast(FP8X4),
                scales=key_scales[:].rearrange("p g j n -> p (g j n)"),
                in_=key_words[c][:].rearrange("p g j n u -> p (g j n u)").bitcast(BF16),
            )
            key_quantised[c] = (key_codes, key_scales)

        def quantise_magnitudes(c):
            tiles = len(groups[c])
            mag_codes = codes.tile([P, tiles, P], U32, align_bytes=64)
            mag_scales = codes.tile([P, tiles, P], U8, align_bytes=64)
            nc.vector.quantize_mx(
                out=mag_codes[:].rearrange("p j n -> p (j n)").bitcast(FP8X4),
                scales=mag_scales[:].rearrange("p j n -> p (j n)"),
                in_=magnitude[c][:].rearrange("p j n t -> p (j n t)"),
            )
            mag_quantised[c] = (mag_codes, mag_scales)

        def multiply_group(c):
            key_codes, key_scales = key_quantised[c]
            mag_codes, mag_scales = mag_quantised[c]
            tiles = len(groups[c])
            acc = psum_out.tile([P, tiles, BINS], F32)
            for j in range(tiles):
                for g in range(2):
                    nc.tensor.matmul_mx(
                        out=acc[:, j, :],
                        lhsT=key_codes[:, g, j, :].bitcast(FP8X4),
                        lhsT_scale=key_scales[:, g, j, :],
                        rhs=rot_codes[:, g, :].bitcast(FP8X4),
                        rhs_scale=rot_scales[:, g, :],
                        start=(g == 0),
                        stop=False,
                    )
                nc.tensor.matmul_mx(
                    out=acc[:, j, :],
                    lhsT=mag_codes[:, j, :].bitcast(FP8X4),
                    lhsT_scale=mag_scales[:, j, :],
                    rhs=w_codes[:].bitcast(FP8X4),
                    rhs_scale=w_scales[:],
                    start=False,
                    stop=True,
                )
            products[c] = acc

        def store_group(c):
            first, tiles = groups[c][0], len(groups[c])
            logits = work.tile([P, tiles, BINS], F32)
            nc.vector.tensor_tensor(
                out=logits[:],
                in0=products[c][:],
                in1=bias_sb[:].unsqueeze(1).to_broadcast([P, tiles, BINS]),
                op=ALU.add,
            )
            nc.sync.dma_start(out=out_dram[:, first : first + tiles, :], in_=logits[:])

        def tile_at(i, lag):
            return i - lag if 0 <= i - lag < ROW_TILES else None

        groups_at = {}
        previous = FIRST_PRODUCT - 1
        for c, group in enumerate(groups):
            last = group[-1]
            groups_at.setdefault((quantise_keys, last + QUANTISE_KEYS), []).append(c)
            groups_at.setdefault((quantise_magnitudes, last + QUANTISE_MAGNITUDES), []).append(c)
            previous = max(last + MULTIPLY, previous + 1)
            groups_at.setdefault((multiply_group, previous), []).append(c)
            groups_at.setdefault((store_group, previous + STORE - MULTIPLY), []).append(c)

        def groups_do(stage, i):
            for c in groups_at.get((stage, i), []):
                stage(c)

        def next_small_step():
            if small_steps:
                small_steps.pop(0)()

        for r in range(GPSIMD_AHEAD):
            square_on_gpsimd(r)
        for i in range(ROW_TILES + STORE + 8):
            if tile_at(i, 0) is not None:
                square_on_scalar(i)
            if tile_at(i, -GPSIMD_AHEAD) is not None:
                square_on_gpsimd(i + GPSIMD_AHEAD)
            if i == 0:
                for k in range(4):
                    next_small_step()
                sum_probe_squares()
            if i == 2:
                take_norm()
            if tile_at(i, 0) is not None:
                transpose_keys(i)
            groups_do(quantise_magnitudes, i)
            if i == 2:
                add_eps()
            if tile_at(i, COPY) is not None:
                copy_keys(i - COPY)
            if i == 2:
                invert_norm()
            else:
                next_small_step()
            groups_do(store_group, i)
            if i == 3:
                for a in range(4):
                    scale_probes(a)
            groups_do(quantise_keys, i)
            if (quantise_keys, i) in groups_at:
                next_small_step()
            if tile_at(i, ROOT) is not None:
                take_roots(i - ROOT)
            if tile_at(i, TRANSPOSE) is not None:
                transpose_squares(i - TRANSPOSE)
            if i == 6:
                transpose_probes()
            if i == 8:
                rotate_half_of_probes(0, re_cos, re_sin)
            if i == 8:
                rotate_half_of_probes(1, im_cos, im_sin)
            if 9 <= i < 11:
                for part in range(2):
                    combine_probes(i - 9, part)
            if i == 13:
                quantise_probes()
            groups_do(multiply_group, i)
